import numpy as np
import ml_dtypes


def mxq(x, axis, fmt="e4m3"):
    dtype, down = {"e4m3": (ml_dtypes.float8_e4m3fn, 7), "e5m2": (ml_dtypes.float8_e5m2, 14)}[fmt]
    v = np.moveaxis(np.asarray(x, np.float32).astype(ml_dtypes.bfloat16).astype(np.float64), axis, -1)
    blocks = v.reshape(v.shape[:-1] + (-1, 32))
    amax = np.abs(blocks).max(-1, keepdims=True)
    byte = np.maximum(np.where(amax > 0, np.frexp(amax)[1] - 1 + 127, 0) - down, 1)
    scale = np.exp2(byte - 127.0)
    codes = (blocks / scale).astype(np.float32).astype(dtype).astype(np.float64)
    return np.moveaxis((codes * scale).reshape(v.shape), -1, axis)


WIDE = False


def mx_kscale(k, group=512):
    if not WIDE:
        return np.ones(k)
    levels = np.array([10, -10, 5, -5, 0])
    if group != 512:
        return np.exp2(np.random.permutation(np.resize(levels, k // group))).repeat(group)
    a = np.random.permutation(np.resize(levels, k // 512 * 4)).reshape(k // 512, 4)
    idx = np.arange(k)
    return np.exp2(a[idx // 512, idx % 128 // 32])


BF16 = ml_dtypes.bfloat16


def bf(x):
    return np.asarray(x, np.float32).astype(BF16)


def f64(x):
    return np.asarray(x).astype(np.float64)


B, C, H, W, KERNEL, M, O = 256, 4, 18, 34, 3, 256, 128
K = C * KERNEL * KERNEL
HO, WO = H - KERNEL + 1, W - KERNEL + 1
L = HO * WO


def unfold(x):
    cols = [x[:, :, i:i + HO, j:j + WO] for i in range(KERNEL) for j in range(KERNEL)]
    return np.stack(cols, axis=2).reshape(B, K, L)


def setup_inputs():
    t = mx_kscale(M, group=M // 2)
    return {"x": bf(np.random.standard_normal((B, C, H, W))),
            "G": bf(np.random.standard_normal((M, L)) / np.sqrt(L) * t[:, None]),
            "v": bf(np.random.standard_normal((M, K, O)) * 0.7 / np.sqrt(K * M) / t[:, None, None]),
            "w": bf(np.random.standard_normal((M, K, O)) * 0.7 / np.sqrt(K * M) / t[:, None, None])}


def reference(x, G, v, w):
    U = unfold(f64(x))
    A = mxq(U, 2, "e4m3") @ mxq(f64(G), 1, "e4m3").T
    p_diff = f64(v) - f64(w)
    return mxq(A.reshape(B, K * M), 1, "e4m3") @ mxq(p_diff.transpose(1, 0, 2).reshape(K * M, O), 0, "e4m3")

@@ -1,0 +1,302 @@
+from contextlib import ExitStack
+
+import concourse.mybir as mybir
+from concourse.masks import make_identity
+
+BF16 = mybir.dt.bfloat16
+F32 = mybir.dt.float32
+U32 = mybir.dt.uint32
+U8 = mybir.dt.uint8
+FP8X4 = mybir.dt.float8_e4m3fn_x4
+
+P = 128
+B, C, H, W = 256, 4, 18, 34
+KERNEL = 3
+HO, WO = H - KERNEL + 1, W - KERNEL + 1
+L = HO * WO
+M, O = 256, 128
+K = C * KERNEL * KERNEL
+FLOPS = 2 * B * K * L * M + 2 * B * K * M * O
+
+HALVES = 2
+ROW_TILES = 4
+COLS = ROW_TILES * P
+M_TILES = M // P
+SHIFTS = KERNEL * KERNEL
+SLOTS = HALVES * SHIFTS
+UNITS = HALVES * KERNEL
+
+WORDS = L // 2
+ROW_WORDS = WO // 2
+
+G_PLAIN, G_DOWN, G_LAST = 0, 1, 2
+TOP, BOTTOM = 0, 1
+
+
+def tile_convexrelucnn_t_kernel(tc, x, G, v, w, out):
+    nc = tc.nc
+
+    with ExitStack() as pools:
+        keep = pools.enter_context(tc.tile_pool(name="keep", bufs=1))
+        work = pools.enter_context(tc.tile_pool(name="work", bufs=2))
+        flip = pools.enter_context(tc.psum_pool(name="flip", bufs=2))
+        first = pools.enter_context(tc.psum_pool(name="first", bufs=4))
+        second = pools.enter_context(tc.psum_pool(name="second", bufs=1))
+
+        x_sb = keep.tile([P, HALVES * ROW_TILES, H * W], BF16)
+        g_pad = keep.tile([P, M_TILES, WO + L], BF16)
+        g_last = keep.tile([P, M_TILES, L], BF16)
+        g_grouped = keep.tile([P, 3, M_TILES * P * 4], BF16, align_bytes=64)
+        g_codes = keep.tile([P, 3, M_TILES * P], U32, align_bytes=64)
+        g_scales = keep.tile([P, 3, M_TILES * P], U8, align_bytes=64)
+        v_sb = keep.tile([P, M_TILES, K, O], BF16)
+        w_sb = keep.tile([P, M_TILES, K, O], BF16)
+        p_codes = keep.tile([P, M_TILES, SHIFTS, O], U32, align_bytes=64)
+        p_scales = keep.tile([P, M_TILES, SHIFTS, O], U8, align_bytes=64)
+        a_codes = keep.tile([P, HALVES, SHIFTS, M_TILES * P], U32, align_bytes=64)
+        a_scales = keep.tile([P, HALVES, SHIFTS, M_TILES * P], U8, align_bytes=64)
+        ident = keep.tile([P, P], F32)
+        acc = [
+            second.tile([P, O], F32, name="acc%d" % half) for half in range(HALVES)
+        ]
+
+        x_rows = x.rearrange("b c h w -> (b c) (h w)").rearrange(
+            "(t p) f -> p t f", p=P
+        )
+
+        def load_x(half):
+            tiles = slice(half * ROW_TILES, (half + 1) * ROW_TILES)
+            nc.sync.dma_start(out=x_sb[:, tiles, :], in_=x_rows[:, tiles, :])
+
+        def load_vw(mt, i):
+            for dram, sbuf in ((v, v_sb), (w, w_sb)):
+                nc.sync.dma_start(
+                    out=sbuf[:, mt].rearrange(
+                        "p (c i r) o -> p c i (r o)", c=C, i=KERNEL
+                    )[:, :, i, :],
+                    in_=dram[mt * P : (mt + 1) * P].rearrange(
+                        "p (c i r) o -> p c i (r o)", c=C, i=KERNEL
+                    )[:, :, i, :],
+                )
+
+        nc.scalar.dma_start(
+            out=g_pad[:, :, WO:], in_=G.rearrange("(t p) n -> p t n", p=P)
+        )
+        load_x(0)
+        for i in range(KERNEL):
+            load_vw(0, i)
+        load_x(1)
+        for i in range(KERNEL):
+            load_vw(1, i)
+
+        make_identity(nc, ident[:])
+
+        def flip_words(words, bank):
+            for r in range(2):
+                for u in range(2):
+                    nc.tensor.transpose(bank[:, r, u, :], words(r, u), ident[:])
+
+        def leave_flip_bank(bank, grouped_words):
+            nc.scalar.copy(
+                out=grouped_words, in_=bank[:].rearrange("p r u c -> p r c u")
+            )
+
+        def prepare_g():
+            nc.vector.memset(g_pad[:, :, :WO], 0.0)
+            nc.vector.memset(g_last[:], 0.0)
+            nc.vector.tensor_copy(
+                out=g_last[:, :, L - 2 * WO : L - WO], in_=g_pad[:, :, L : L + WO]
+            )
+            pad_words = g_pad[:].bitcast(F32)
+            last_words = g_last[:].bitcast(F32)
+            sources = {
+                G_PLAIN: (pad_words, ROW_WORDS),
+                G_DOWN: (pad_words, 0),
+                G_LAST: (last_words, 0),
+            }
+            for form in (G_PLAIN, G_DOWN, G_LAST):
+                source, start = sources[form]
+                bank = flip.tile([P, 2, 2, P], F32, name="bank")
+                flip_words(
+                    lambda mt, u: source[:, mt, start + u * P : start + (u + 1) * P],
+                    bank,
+                )
+                leave_flip_bank(
+                    bank,
+                    g_grouped[:, form, :]
+                    .bitcast(F32)
+                    .rearrange("p (r c u) -> p r c u", r=2, u=2),
+                )
+
+        def quantise_g():
+            for form in (G_PLAIN, G_DOWN, G_LAST):
+                nc.vector.quantize_mx(
+                    out=g_codes[:, form, :].bitcast(FP8X4),
+                    scales=g_scales[:, form, :],
+                    in_=g_grouped[:, form, :],
+                )
+
+        packed = {}
+        u_grouped = {}
+        u_mx = {}
+
+        def pack_rows(unit):
+            half, j = divmod(unit, KERNEL)
+            tiles = slice(half * ROW_TILES, (half + 1) * ROW_TILES)
+            rows = work.tile([P, ROW_TILES, H * WO], BF16, name="rows")
+            nc.vector.tensor_copy(
+                out=rows[:].rearrange("p t (h w) -> p t h w", w=WO),
+                in_=x_sb[:, tiles, :].rearrange("p t (h w) -> p t h w", w=W)[
+                    :, :, :, j : j + WO
+                ],
+            )
+            packed[unit] = rows
+
+        def flip_u(unit, window):
+            row_words = packed[unit][:].bitcast(F32)
+            start = 2 * window * ROW_WORDS
+            grouped = work.tile([P, COLS * 4], BF16, name="grouped", align_bytes=64)
+            grouped_words = grouped[:].bitcast(F32).rearrange(
+                "p (t c u) -> p t c u", t=ROW_TILES, u=2
+            )
+            banks = []
+            for pair in range(ROW_TILES // 2):
+                bank = flip.tile([P, 2, 2, P], F32, name="bank")
+                flip_words(
+                    lambda r, u: row_words[
+                        :, 2 * pair + r, start + u * P : start + (u + 1) * P
+                    ],
+                    bank,
+                )
+                banks.append(bank)
+            u_grouped[(unit, window)] = grouped
+            return [
+                (banks[pair], grouped_words[:, 2 * pair : 2 * pair + 2, :, :])
+                for pair in range(ROW_TILES // 2)
+            ]
+
+        def quantise_u(unit, window):
+            codes = work.tile([P, COLS], U32, name="u_codes%d" % window, align_bytes=64)
+            scales = work.tile([P, COLS], U8, name="u_scales%d" % window, align_bytes=64)
+            nc.vector.quantize_mx(
+                out=codes[:].bitcast(FP8X4),
+                scales=scales[:],
+                in_=u_grouped[(unit, window)][:],
+            )
+            u_mx[(unit, window)] = (codes, scales)
+
+        def first_pass(bank, form, mt, unit, window, start, stop):
+            codes, scales = u_mx[(unit, window)]
+            m_cols = slice(mt * P, (mt + 1) * P)
+            nc.tensor.matmul_mx(
+                out=bank[:],
+                lhsT=g_codes[:, form, m_cols].bitcast(FP8X4),
+                lhsT_scale=g_scales[:, form, m_cols],
+                rhs=codes[:].bitcast(FP8X4),
+                rhs_scale=scales[:],
+                start=start,
+                stop=stop,
+            )
+
+        def first_matmul(unit, i):
+            banks = []
+            for mt in range(M_TILES):
+                bank = first.tile([P, COLS], F32, name="a_bank")
+                if i == 0:
+                    first_pass(bank, G_PLAIN, mt, unit, TOP, True, True)
+                elif i == 1:
+                    first_pass(bank, G_DOWN, mt, unit, TOP, True, False)
+                    first_pass(bank, G_LAST, mt, unit, BOTTOM, False, True)
+                else:
+                    first_pass(bank, G_PLAIN, mt, unit, BOTTOM, True, True)
+                banks.append(bank)
+            return banks
+
+        def channels_of(sbuf, mt, i, j):
+            return sbuf[:, mt].rearrange("p (c r) o -> p c r o", c=C)[
+                :, :, i * KERNEL + j, :
+            ]
+
+        def second_pass(half, shift, mt, start, stop):
+            m_cols = slice(mt * P, (mt + 1) * P)
+            nc.tensor.matmul_mx(
+                out=acc[half][:],
+                lhsT=a_codes[:, half, shift, m_cols].bitcast(FP8X4),
+                lhsT_scale=a_scales[:, half, shift, m_cols],
+                rhs=p_codes[:, mt, shift, :].bitcast(FP8X4),
+                rhs_scale=p_scales[:, mt, shift, :],
+                start=start,
+                stop=stop,
+            )
+
+        def second_matmul(slot):
+            half, shift = divmod(slot, SHIFTS)
+            opens, closes = shift == 0, shift == SHIFTS - 1
+            if half == 0:
+                second_pass(0, shift, 0, opens, False)
+            else:
+                second_pass(0, shift, 1, False, closes)
+                second_pass(1, shift, 0, opens, False)
+                second_pass(1, shift, 1, False, closes)
+
+        prepare_g()
+        pack_rows(0)
+        for window in (TOP, BOTTOM):
+            for bank, grouped_words in flip_u(0, window):
+                leave_flip_bank(bank, grouped_words)
+        quantise_g()
+        quantise_u(0, TOP)
+        quantise_u(0, BOTTOM)
+        pack_rows(1)
+
+        for slot in range(SLOTS):
+            unit, i = divmod(slot, KERNEL)
+            half, shift = divmod(slot, SHIFTS)
+            j = unit % KERNEL
+            builds = i < 2 and unit + 1 < UNITS
+
+            a_banks = first_matmul(unit, i)
+            flipped = flip_u(unit + 1, i) if builds else []
+            if slot > 0:
+                second_matmul(slot - 1)
+
+            a_bf = work.tile([P, M_TILES, COLS], BF16, name="a_bf", align_bytes=64)
+            for mt in range(M_TILES):
+                nc.scalar.copy(out=a_bf[:, mt, :], in_=a_banks[mt][:])
+            for bank, grouped_words in flipped:
+                leave_flip_bank(bank, grouped_words)
+
+            p_mt = half
+            diff = work.tile([P, C, O], BF16, name="diff")
+            nc.vector.tensor_tensor(
+                out=diff[:],
+                in0=channels_of(v_sb, p_mt, i, j),
+                in1=channels_of(w_sb, p_mt, i, j),
+                op=mybir.AluOpType.subtract,
+            )
+            nc.vector.quantize_mx(
+                out=a_codes[:, half, shift, :].bitcast(FP8X4),
+                scales=a_scales[:, half, shift, :],
+                in_=a_bf[:].rearrange("p t c -> p (t c)"),
+            )
+            p_grouped = work.tile([P, O, C], BF16, name="p_grouped", align_bytes=64)
+            nc.vector.tensor_copy(
+                out=p_grouped[:].rearrange("p (q r) c -> p q c r", r=4),
+                in_=diff[:].rearrange("p c (q r) -> p q c r", r=4),
+            )
+            if builds:
+                quantise_u(unit + 1, i)
+            elif unit + 2 < UNITS:
+                pack_rows(unit + 2)
+            nc.vector.quantize_mx(
+                out=p_codes[:, p_mt, shift, :].bitcast(FP8X4),
+                scales=p_scales[:, p_mt, shift, :],
+                in_=p_grouped[:].rearrange("p o c -> p (o c)"),
+            )
+
+        second_matmul(SLOTS - 1)
+
+        for half in range(HALVES):
+            result = work.tile([P, O], F32, name="result")
+            nc.scalar.copy(out=result[:], in_=acc[half][:])
+            nc.sync.dma_start(out=out[half * P : (half + 1) * P, :], in_=result[:])

@@ -29,6 +29,8 @@ UNITS = HALVES * KERNEL
 WORDS = L // 2
 ROW_WORDS = WO // 2
 
+SECOND_LAG = 2
+
 G_PLAIN, G_DOWN, G_LAST = 0, 1, 2
 TOP, BOTTOM = 0, 1
 
@@ -96,10 +98,12 @@ def tile_convexrelucnn_t_kernel(tc, x, G, v, w, out):
                 for u in range(2):
                     nc.tensor.transpose(bank[:, r, u, :], words(r, u), ident[:])
 
-        def leave_flip_bank(bank, grouped_words):
-            nc.scalar.copy(
-                out=grouped_words, in_=bank[:].rearrange("p r u c -> p r c u")
-            )
+        def leave_flip_bank(bank, grouped_words, on_vector=False):
+            side_by_side = bank[:].rearrange("p r u c -> p r c u")
+            if on_vector:
+                nc.vector.tensor_copy(out=grouped_words, in_=side_by_side)
+            else:
+                nc.scalar.copy(out=grouped_words, in_=side_by_side)
 
         def prepare_g():
             nc.vector.memset(g_pad[:, :, :WO], 0.0)
@@ -198,7 +202,8 @@ def tile_convexrelucnn_t_kernel(tc, x, G, v, w, out):
                 stop=stop,
             )
 
-        def first_matmul(unit, i):
+        def first_matmul(slot):
+            unit, i = divmod(slot, KERNEL)
             banks = []
             for mt in range(M_TILES):
                 bank = first.tile([P, COLS], F32, name="a_bank")
@@ -239,64 +244,71 @@ def tile_convexrelucnn_t_kernel(tc, x, G, v, w, out):
                 second_pass(1, shift, 0, opens, False)
                 second_pass(1, shift, 1, False, closes)
 
-        prepare_g()
-        pack_rows(0)
-        for window in (TOP, BOTTOM):
-            for bank, grouped_words in flip_u(0, window):
-                leave_flip_bank(bank, grouped_words)
-        quantise_g()
-        quantise_u(0, TOP)
-        quantise_u(0, BOTTOM)
-        pack_rows(1)
+        with tc.manual_schedule():
+            prepare_g()
+            pack_rows(0)
+            quantise_g()
+            for window in (TOP, BOTTOM):
+                for pair, (bank, grouped_words) in enumerate(flip_u(0, window)):
+                    leave_flip_bank(bank, grouped_words, on_vector=(pair == 1))
+                quantise_u(0, window)
+            pack_rows(1)
+            a_banks = {0: first_matmul(0)}
 
-        for slot in range(SLOTS):
-            unit, i = divmod(slot, KERNEL)
-            half, shift = divmod(slot, SHIFTS)
-            j = unit % KERNEL
-            builds = i < 2 and unit + 1 < UNITS
+            for slot in range(SLOTS):
+                unit, i = divmod(slot, KERNEL)
+                half, shift = divmod(slot, SHIFTS)
+                j = unit % KERNEL
+                builds = i < 2 and unit + 1 < UNITS
 
-            a_banks = first_matmul(unit, i)
-            flipped = flip_u(unit + 1, i) if builds else []
-            if slot > 0:
-                second_matmul(slot - 1)
+                if slot + 1 < SLOTS:
+                    a_banks[slot + 1] = first_matmul(slot + 1)
+                flipped = flip_u(unit + 1, i) if builds else []
+                if slot >= SECOND_LAG:
+                    second_matmul(slot - SECOND_LAG)
 
-            a_bf = work.tile([P, M_TILES, COLS], BF16, name="a_bf", align_bytes=64)
-            for mt in range(M_TILES):
-                nc.scalar.copy(out=a_bf[:, mt, :], in_=a_banks[mt][:])
-            for bank, grouped_words in flipped:
-                leave_flip_bank(bank, grouped_words)
+                a_bf = work.tile(
+                    [P, M_TILES, COLS], BF16, name="a_bf", bufs=4, align_bytes=64
+                )
+                for mt in range(M_TILES):
+                    nc.scalar.copy(out=a_bf[:, mt, :], in_=a_banks[slot][mt][:])
+                for bank, grouped_words in flipped:
+                    leave_flip_bank(bank, grouped_words)
 
-            p_mt = half
-            diff = work.tile([P, C, O], BF16, name="diff")
-            nc.vector.tensor_tensor(
-                out=diff[:],
-                in0=channels_of(v_sb, p_mt, i, j),
-                in1=channels_of(w_sb, p_mt, i, j),
-                op=mybir.AluOpType.subtract,
-            )
-            nc.vector.quantize_mx(
-                out=a_codes[:, half, shift, :].bitcast(FP8X4),
-                scales=a_scales[:, half, shift, :],
-                in_=a_bf[:].rearrange("p t c -> p (t c)"),
-            )
-            p_grouped = work.tile([P, O, C], BF16, name="p_grouped", align_bytes=64)
-            nc.vector.tensor_copy(
-                out=p_grouped[:].rearrange("p (q r) c -> p q c r", r=4),
-                in_=diff[:].rearrange("p c (q r) -> p q c r", r=4),
-            )
-            if builds:
-                quantise_u(unit + 1, i)
-            elif unit + 2 < UNITS:
-                pack_rows(unit + 2)
-            nc.vector.quantize_mx(
-                out=p_codes[:, p_mt, shift, :].bitcast(FP8X4),
-                scales=p_scales[:, p_mt, shift, :],
-                in_=p_grouped[:].rearrange("p o c -> p (o c)"),
-            )
+                p_mt = half
+                diff = work.tile([P, C, O], BF16, name="diff")
+                nc.vector.tensor_tensor(
+                    out=diff[:],
+                    in0=channels_of(v_sb, p_mt, i, j),
+                    in1=channels_of(w_sb, p_mt, i, j),
+                    op=mybir.AluOpType.subtract,
+                )
+                nc.vector.quantize_mx(
+                    out=a_codes[:, half, shift, :].bitcast(FP8X4),
+                    scales=a_scales[:, half, shift, :],
+                    in_=a_bf[:].rearrange("p t c -> p (t c)"),
+                )
+                p_grouped = work.tile([P, O, C], BF16, name="p_grouped", align_bytes=64)
+                nc.vector.tensor_copy(
+                    out=p_grouped[:].rearrange("p (q r) c -> p q c r", r=4),
+                    in_=diff[:].rearrange("p c (q r) -> p q c r", r=4),
+                )
+                if builds:
+                    quantise_u(unit + 1, i)
+                elif unit + 2 < UNITS:
+                    pack_rows(unit + 2)
+                nc.vector.quantize_mx(
+                    out=p_codes[:, p_mt, shift, :].bitcast(FP8X4),
+                    scales=p_scales[:, p_mt, shift, :],
+                    in_=p_grouped[:].rearrange("p o c -> p (o c)"),
+                )
 
-        second_matmul(SLOTS - 1)
+            for slot in range(SLOTS - SECOND_LAG, SLOTS):
+                second_matmul(slot)
 
-        for half in range(HALVES):
-            result = work.tile([P, O], F32, name="result")
-            nc.scalar.copy(out=result[:], in_=acc[half][:])
-            nc.sync.dma_start(out=out[half * P : (half + 1) * P, :], in_=result[:])
+            result0 = work.tile([P, O], F32, name="result0")
+            result1 = work.tile([P, O], F32, name="result1")
+            nc.scalar.copy(out=result0[:], in_=acc[0][:])
+            nc.vector.tensor_copy(out=result1[:], in_=acc[1][:])
+            nc.sync.dma_start(out=out[:P, :], in_=result0[:])
+            nc.sync.dma_start(out=out[P:, :], in_=result1[:])

@@ -22,14 +22,9 @@ HALVES = 2
 ROW_TILES = 4
 COLS = ROW_TILES * P
 M_TILES = M // P
-SHIFTS = KERNEL * KERNEL
-SLOTS = HALVES * SHIFTS
 UNITS = HALVES * KERNEL
-
-WORDS = L // 2
+BANK = 512
 ROW_WORDS = WO // 2
-
-SECOND_LAG = 2
 
 G_PLAIN, G_DOWN, G_LAST = 0, 1, 2
 TOP, BOTTOM = 0, 1
@@ -41,11 +36,11 @@ def tile_convexrelucnn_t_kernel(tc, x, G, v, w, out):
     with ExitStack() as pools:
         keep = pools.enter_context(tc.tile_pool(name="keep", bufs=1))
         work = pools.enter_context(tc.tile_pool(name="work", bufs=2))
-        flip = pools.enter_context(tc.psum_pool(name="flip", bufs=2))
-        first = pools.enter_context(tc.psum_pool(name="first", bufs=4))
-        second = pools.enter_context(tc.psum_pool(name="second", bufs=1))
+        banks = pools.enter_context(tc.psum_pool(name="banks", bufs=6))
+        sums = pools.enter_context(tc.psum_pool(name="sums", bufs=1))
 
         x_sb = keep.tile([P, HALVES * ROW_TILES, H * W], BF16)
+        rows = keep.tile([P, UNITS, ROW_TILES, H * WO], BF16)
         g_pad = keep.tile([P, M_TILES, WO + L], BF16)
         g_last = keep.tile([P, M_TILES, L], BF16)
         g_grouped = keep.tile([P, 3, M_TILES * P * 4], BF16, align_bytes=64)
@@ -53,64 +48,52 @@ def tile_convexrelucnn_t_kernel(tc, x, G, v, w, out):
         g_scales = keep.tile([P, 3, M_TILES * P], U8, align_bytes=64)
         v_sb = keep.tile([P, M_TILES, K, O], BF16)
         w_sb = keep.tile([P, M_TILES, K, O], BF16)
-        p_codes = keep.tile([P, M_TILES, SHIFTS, O], U32, align_bytes=64)
-        p_scales = keep.tile([P, M_TILES, SHIFTS, O], U8, align_bytes=64)
-        a_codes = keep.tile([P, HALVES, SHIFTS, M_TILES * P], U32, align_bytes=64)
-        a_scales = keep.tile([P, HALVES, SHIFTS, M_TILES * P], U8, align_bytes=64)
+        p_codes = keep.tile([P, M_TILES, KERNEL, KERNEL, O], U32, align_bytes=64)
+        p_scales = keep.tile([P, M_TILES, KERNEL, KERNEL, O], U8, align_bytes=64)
+        a_codes = keep.tile([P, UNITS, KERNEL, M_TILES * P], U32, align_bytes=64)
+        a_scales = keep.tile([P, UNITS, KERNEL, M_TILES * P], U8, align_bytes=64)
         ident = keep.tile([P, P], F32)
-        acc = [
-            second.tile([P, O], F32, name="acc%d" % half) for half in range(HALVES)
-        ]
+        acc = [sums.tile([P, O], F32, name="acc%d" % half) for half in range(HALVES)]
 
         x_rows = x.rearrange("b c h w -> (b c) (h w)").rearrange(
             "(t p) f -> p t f", p=P
         )
-
-        def load_x(half):
+        for half in range(HALVES):
             tiles = slice(half * ROW_TILES, (half + 1) * ROW_TILES)
             nc.sync.dma_start(out=x_sb[:, tiles, :], in_=x_rows[:, tiles, :])
-
-        def load_vw(mt, i):
-            for dram, sbuf in ((v, v_sb), (w, w_sb)):
-                nc.sync.dma_start(
-                    out=sbuf[:, mt].rearrange(
-                        "p (c i r) o -> p c i (r o)", c=C, i=KERNEL
-                    )[:, :, i, :],
-                    in_=dram[mt * P : (mt + 1) * P].rearrange(
-                        "p (c i r) o -> p c i (r o)", c=C, i=KERNEL
-                    )[:, :, i, :],
+            if half == 0:
+                nc.scalar.dma_start(
+                    out=g_pad[:, :, WO:], in_=G.rearrange("(t p) n -> p t n", p=P)
                 )
-
-        nc.scalar.dma_start(
-            out=g_pad[:, :, WO:], in_=G.rearrange("(t p) n -> p t n", p=P)
-        )
-        load_x(0)
-        for i in range(KERNEL):
-            load_vw(0, i)
-        load_x(1)
-        for i in range(KERNEL):
-            load_vw(1, i)
+        for mt in range(M_TILES):
+            nc.sync.dma_start(out=v_sb[:, mt], in_=v[mt * P : (mt + 1) * P])
+            nc.sync.dma_start(out=w_sb[:, mt], in_=w[mt * P : (mt + 1) * P])
 
         make_identity(nc, ident[:])
 
-        def flip_words(words, bank):
+        def flip_words(words):
+            bank = banks.tile([P, BANK], F32, name="bank")
+            blocks = bank[:].rearrange("p (r u c) -> p r u c", r=2, u=2)
             for r in range(2):
                 for u in range(2):
-                    nc.tensor.transpose(bank[:, r, u, :], words(r, u), ident[:])
+                    nc.tensor.transpose(blocks[:, r, u, :], words(r, u), ident[:])
+            return blocks
 
-        def leave_flip_bank(bank, grouped_words, on_vector=False):
-            side_by_side = bank[:].rearrange("p r u c -> p r c u")
-            if on_vector:
-                nc.vector.tensor_copy(out=grouped_words, in_=side_by_side)
-            else:
-                nc.scalar.copy(out=grouped_words, in_=side_by_side)
+        def leave_flip_bank(blocks, grouped_words):
+            nc.scalar.copy(
+                out=grouped_words, in_=blocks.rearrange("p r u c -> p r c u")
+            )
 
-        def prepare_g():
+        def zero_g():
             nc.vector.memset(g_pad[:, :, :WO], 0.0)
             nc.vector.memset(g_last[:], 0.0)
+
+        def fill_g_last():
             nc.vector.tensor_copy(
                 out=g_last[:, :, L - 2 * WO : L - WO], in_=g_pad[:, :, L : L + WO]
             )
+
+        def build_g():
             pad_words = g_pad[:].bitcast(F32)
             last_words = g_last[:].bitcast(F32)
             sources = {
@@ -120,19 +103,15 @@ def tile_convexrelucnn_t_kernel(tc, x, G, v, w, out):
             }
             for form in (G_PLAIN, G_DOWN, G_LAST):
                 source, start = sources[form]
-                bank = flip.tile([P, 2, 2, P], F32, name="bank")
-                flip_words(
-                    lambda mt, u: source[:, mt, start + u * P : start + (u + 1) * P],
-                    bank,
+                blocks = flip_words(
+                    lambda mt, u: source[:, mt, start + u * P : start + (u + 1) * P]
                 )
                 leave_flip_bank(
-                    bank,
+                    blocks,
                     g_grouped[:, form, :]
                     .bitcast(F32)
                     .rearrange("p (r c u) -> p r c u", r=2, u=2),
                 )
-
-        def quantise_g():
             for form in (G_PLAIN, G_DOWN, G_LAST):
                 nc.vector.quantize_mx(
                     out=g_codes[:, form, :].bitcast(FP8X4),
@@ -140,52 +119,36 @@ def tile_convexrelucnn_t_kernel(tc, x, G, v, w, out):
                     in_=g_grouped[:, form, :],
                 )
 
-        packed = {}
-        u_grouped = {}
         u_mx = {}
 
         def pack_rows(unit):
             half, j = divmod(unit, KERNEL)
             tiles = slice(half * ROW_TILES, (half + 1) * ROW_TILES)
-            rows = work.tile([P, ROW_TILES, H * WO], BF16, name="rows")
             nc.vector.tensor_copy(
-                out=rows[:].rearrange("p t (h w) -> p t h w", w=WO),
+                out=rows[:, unit].rearrange("p t (h w) -> p t h w", w=WO),
                 in_=x_sb[:, tiles, :].rearrange("p t (h w) -> p t h w", w=W)[
                     :, :, :, j : j + WO
                 ],
             )
-            packed[unit] = rows
 
-        def flip_u(unit, window):
-            row_words = packed[unit][:].bitcast(F32)
+        def build_u(unit, window):
+            row_words = rows[:, unit].bitcast(F32)
             start = 2 * window * ROW_WORDS
             grouped = work.tile([P, COLS * 4], BF16, name="grouped", align_bytes=64)
             grouped_words = grouped[:].bitcast(F32).rearrange(
                 "p (t c u) -> p t c u", t=ROW_TILES, u=2
             )
-            banks = []
             for pair in range(ROW_TILES // 2):
-                bank = flip.tile([P, 2, 2, P], F32, name="bank")
-                flip_words(
+                blocks = flip_words(
                     lambda r, u: row_words[
                         :, 2 * pair + r, start + u * P : start + (u + 1) * P
-                    ],
-                    bank,
+                    ]
                 )
-                banks.append(bank)
-            u_grouped[(unit, window)] = grouped
-            return [
-                (banks[pair], grouped_words[:, 2 * pair : 2 * pair + 2, :, :])
-                for pair in range(ROW_TILES // 2)
-            ]
-
-        def quantise_u(unit, window):
+                leave_flip_bank(blocks, grouped_words[:, 2 * pair : 2 * pair + 2, :, :])
             codes = work.tile([P, COLS], U32, name="u_codes%d" % window, align_bytes=64)
             scales = work.tile([P, COLS], U8, name="u_scales%d" % window, align_bytes=64)
             nc.vector.quantize_mx(
-                out=codes[:].bitcast(FP8X4),
-                scales=scales[:],
-                in_=u_grouped[(unit, window)][:],
+                out=codes[:].bitcast(FP8X4), scales=scales[:], in_=grouped[:]
             )
             u_mx[(unit, window)] = (codes, scales)
 
@@ -202,11 +165,10 @@ def tile_convexrelucnn_t_kernel(tc, x, G, v, w, out):
                 stop=stop,
             )
 
-        def first_matmul(slot):
-            unit, i = divmod(slot, KERNEL)
-            banks = []
+        def matmul_a(unit, i):
+            a_bf = work.tile([P, M_TILES, COLS], BF16, name="a_bf", bufs=4, align_bytes=64)
             for mt in range(M_TILES):
-                bank = first.tile([P, COLS], F32, name="a_bank")
+                bank = banks.tile([P, BANK], F32, name="bank")
                 if i == 0:
                     first_pass(bank, G_PLAIN, mt, unit, TOP, True, True)
                 elif i == 1:
@@ -214,97 +176,105 @@ def tile_convexrelucnn_t_kernel(tc, x, G, v, w, out):
                     first_pass(bank, G_LAST, mt, unit, BOTTOM, False, True)
                 else:
                     first_pass(bank, G_PLAIN, mt, unit, BOTTOM, True, True)
-                banks.append(bank)
-            return banks
+                if unit + KERNEL >= UNITS and i == 1 and mt == 1:
+                    nc.vector.tensor_copy(out=a_bf[:, mt, :], in_=bank[:])
+                else:
+                    nc.scalar.copy(out=a_bf[:, mt, :], in_=bank[:])
+            return a_bf
 
-        def channels_of(sbuf, mt, i, j):
-            return sbuf[:, mt].rearrange("p (c r) o -> p c r o", c=C)[
-                :, :, i * KERNEL + j, :
+        def quantise_a(unit, i, a_bf):
+            nc.vector.quantize_mx(
+                out=a_codes[:, unit, i, :].bitcast(FP8X4),
+                scales=a_scales[:, unit, i, :],
+                in_=a_bf[:].rearrange("p t c -> p (t c)"),
+            )
+
+        def rows_of_j(sbuf, mt, j):
+            return sbuf[:, mt].rearrange("p (c i r) o -> p c i r o", c=C, i=KERNEL)[
+                :, :, :, j, :
             ]
 
-        def second_pass(half, shift, mt, start, stop):
+        def subtract_p(unit):
+            mt, j = divmod(unit, KERNEL)
+            diff = work.tile([P, C, KERNEL, O], BF16, name="diff")
+            nc.vector.tensor_tensor(
+                out=diff[:],
+                in0=rows_of_j(v_sb, mt, j),
+                in1=rows_of_j(w_sb, mt, j),
+                op=mybir.AluOpType.subtract,
+            )
+            return diff
+
+        def regroup_p(diff):
+            p_grouped = work.tile([P, KERNEL, O, C], BF16, name="p_grouped", align_bytes=64)
+            nc.vector.tensor_copy(
+                out=p_grouped[:].rearrange("p i (q r) c -> p i q c r", r=4),
+                in_=diff[:].rearrange("p c i (q r) -> p i q c r", r=4),
+            )
+            return p_grouped
+
+        def quantise_p(unit, p_grouped):
+            mt, j = divmod(unit, KERNEL)
+            for i in range(KERNEL):
+                nc.vector.quantize_mx(
+                    out=p_codes[:, mt, j, i, :].bitcast(FP8X4),
+                    scales=p_scales[:, mt, j, i, :],
+                    in_=p_grouped[:, i].rearrange("p o c -> p (o c)"),
+                )
+
+        def second_pass(half, j, i, mt, start, stop):
             m_cols = slice(mt * P, (mt + 1) * P)
             nc.tensor.matmul_mx(
                 out=acc[half][:],
-                lhsT=a_codes[:, half, shift, m_cols].bitcast(FP8X4),
-                lhsT_scale=a_scales[:, half, shift, m_cols],
-                rhs=p_codes[:, mt, shift, :].bitcast(FP8X4),
-                rhs_scale=p_scales[:, mt, shift, :],
+                lhsT=a_codes[:, half * KERNEL + j, i, m_cols].bitcast(FP8X4),
+                lhsT_scale=a_scales[:, half * KERNEL + j, i, m_cols],
+                rhs=p_codes[:, mt, j, i, :].bitcast(FP8X4),
+                rhs_scale=p_scales[:, mt, j, i, :],
                 start=start,
                 stop=stop,
             )
 
-        def second_matmul(slot):
-            half, shift = divmod(slot, SHIFTS)
-            opens, closes = shift == 0, shift == SHIFTS - 1
-            if half == 0:
-                second_pass(0, shift, 0, opens, False)
-            else:
-                second_pass(0, shift, 1, False, closes)
-                second_pass(1, shift, 0, opens, False)
-                second_pass(1, shift, 1, False, closes)
+        def second_matmul(unit):
+            half, j = divmod(unit, KERNEL)
+            for i in range(KERNEL):
+                opens = j == 0 and i == 0
+                closes = j == KERNEL - 1 and i == KERNEL - 1
+                if half == 0:
+                    second_pass(0, j, i, 0, opens, False)
+                else:
+                    second_pass(0, j, i, 1, False, closes)
+                    second_pass(1, j, i, 0, opens, False)
+                    second_pass(1, j, i, 1, False, closes)
 
         with tc.manual_schedule():
-            prepare_g()
+            zero_g()
             pack_rows(0)
-            quantise_g()
-            for window in (TOP, BOTTOM):
-                for pair, (bank, grouped_words) in enumerate(flip_u(0, window)):
-                    leave_flip_bank(bank, grouped_words, on_vector=(pair == 1))
-                quantise_u(0, window)
+            fill_g_last()
             pack_rows(1)
-            a_banks = {0: first_matmul(0)}
+            build_u(0, TOP)
+            build_g()
+            build_u(0, BOTTOM)
+            pack_rows(2)
 
-            for slot in range(SLOTS):
-                unit, i = divmod(slot, KERNEL)
-                half, shift = divmod(slot, SHIFTS)
-                j = unit % KERNEL
-                builds = i < 2 and unit + 1 < UNITS
-
-                if slot + 1 < SLOTS:
-                    a_banks[slot + 1] = first_matmul(slot + 1)
-                flipped = flip_u(unit + 1, i) if builds else []
-                if slot >= SECOND_LAG:
-                    second_matmul(slot - SECOND_LAG)
-
-                a_bf = work.tile(
-                    [P, M_TILES, COLS], BF16, name="a_bf", bufs=4, align_bytes=64
-                )
-                for mt in range(M_TILES):
-                    nc.scalar.copy(out=a_bf[:, mt, :], in_=a_banks[slot][mt][:])
-                for bank, grouped_words in flipped:
-                    leave_flip_bank(bank, grouped_words)
-
-                p_mt = half
-                diff = work.tile([P, C, O], BF16, name="diff")
-                nc.vector.tensor_tensor(
-                    out=diff[:],
-                    in0=channels_of(v_sb, p_mt, i, j),
-                    in1=channels_of(w_sb, p_mt, i, j),
-                    op=mybir.AluOpType.subtract,
-                )
-                nc.vector.quantize_mx(
-                    out=a_codes[:, half, shift, :].bitcast(FP8X4),
-                    scales=a_scales[:, half, shift, :],
-                    in_=a_bf[:].rearrange("p t c -> p (t c)"),
-                )
-                p_grouped = work.tile([P, O, C], BF16, name="p_grouped", align_bytes=64)
-                nc.vector.tensor_copy(
-                    out=p_grouped[:].rearrange("p (q r) c -> p q c r", r=4),
-                    in_=diff[:].rearrange("p c (q r) -> p q c r", r=4),
-                )
-                if builds:
-                    quantise_u(unit + 1, i)
-                elif unit + 2 < UNITS:
-                    pack_rows(unit + 2)
-                nc.vector.quantize_mx(
-                    out=p_codes[:, p_mt, shift, :].bitcast(FP8X4),
-                    scales=p_scales[:, p_mt, shift, :],
-                    in_=p_grouped[:].rearrange("p o c -> p (o c)"),
-                )
-
-            for slot in range(SLOTS - SECOND_LAG, SLOTS):
-                second_matmul(slot)
+            for unit in range(UNITS):
+                a_bf = matmul_a(unit, 0)
+                quantise_a(unit, 0, a_bf)
+                if unit + KERNEL < UNITS:
+                    pack_rows(unit + KERNEL)
+                if unit + 1 < UNITS:
+                    build_u(unit + 1, TOP)
+                diff = subtract_p(unit)
+                if unit + 1 < UNITS:
+                    build_u(unit + 1, BOTTOM)
+                p_grouped = regroup_p(diff)
+                if unit > 0:
+                    second_matmul(unit - 1)
+                a_bf = matmul_a(unit, 1)
+                quantise_p(unit, p_grouped)
+                quantise_a(unit, 1, a_bf)
+                a_bf = matmul_a(unit, 2)
+                quantise_a(unit, 2, a_bf)
+            second_matmul(UNITS - 1)
 
             result0 = work.tile([P, O], F32, name="result0")
             result1 = work.tile([P, O], F32, name="result1")

@@ -58,13 +58,12 @@ def tile_convexrelucnn_t_kernel(tc, x, G, v, w, out):
         x_rows = x.rearrange("b c h w -> (b c) (h w)").rearrange(
             "(t p) f -> p t f", p=P
         )
+        nc.scalar.dma_start(
+            out=g_pad[:, :, WO:], in_=G.rearrange("(t p) n -> p t n", p=P)
+        )
         for half in range(HALVES):
             tiles = slice(half * ROW_TILES, (half + 1) * ROW_TILES)
             nc.sync.dma_start(out=x_sb[:, tiles, :], in_=x_rows[:, tiles, :])
-            if half == 0:
-                nc.scalar.dma_start(
-                    out=g_pad[:, :, WO:], in_=G.rearrange("(t p) n -> p t n", p=P)
-                )
         for mt in range(M_TILES):
             nc.sync.dma_start(out=v_sb[:, mt], in_=v[mt * P : (mt + 1) * P])
             nc.sync.dma_start(out=w_sb[:, mt], in_=w[mt * P : (mt + 1) * P])
@@ -93,7 +92,7 @@ def tile_convexrelucnn_t_kernel(tc, x, G, v, w, out):
                 out=g_last[:, :, L - 2 * WO : L - WO], in_=g_pad[:, :, L : L + WO]
             )
 
-        def build_g():
+        def flip_g():
             pad_words = g_pad[:].bitcast(F32)
             last_words = g_last[:].bitcast(F32)
             sources = {
@@ -112,6 +111,8 @@ def tile_convexrelucnn_t_kernel(tc, x, G, v, w, out):
                     .bitcast(F32)
                     .rearrange("p (r c u) -> p r c u", r=2, u=2),
                 )
+
+        def quantise_g():
             for form in (G_PLAIN, G_DOWN, G_LAST):
                 nc.vector.quantize_mx(
                     out=g_codes[:, form, :].bitcast(FP8X4),
@@ -176,7 +177,7 @@ def tile_convexrelucnn_t_kernel(tc, x, G, v, w, out):
                     first_pass(bank, G_LAST, mt, unit, BOTTOM, False, True)
                 else:
                     first_pass(bank, G_PLAIN, mt, unit, BOTTOM, True, True)
-                if unit + KERNEL >= UNITS and i == 1 and mt == 1:
+                if KERNEL <= unit < UNITS - 1 and i == 1 and mt == 1:
                     nc.vector.tensor_copy(out=a_bf[:, mt, :], in_=bank[:])
                 else:
                     nc.scalar.copy(out=a_bf[:, mt, :], in_=bank[:])
@@ -248,25 +249,25 @@ def tile_convexrelucnn_t_kernel(tc, x, G, v, w, out):
 
         with tc.manual_schedule():
             zero_g()
-            pack_rows(0)
             fill_g_last()
+            flip_g()
+            pack_rows(0)
+            quantise_g()
             pack_rows(1)
             build_u(0, TOP)
-            build_g()
             build_u(0, BOTTOM)
             pack_rows(2)
 
             for unit in range(UNITS):
-                a_bf = matmul_a(unit, 0)
-                quantise_a(unit, 0, a_bf)
                 if unit + KERNEL < UNITS:
                     pack_rows(unit + KERNEL)
+                diff = subtract_p(unit)
+                a_bf = matmul_a(unit, 0)
+                quantise_a(unit, 0, a_bf)
+                p_grouped = regroup_p(diff)
                 if unit + 1 < UNITS:
                     build_u(unit + 1, TOP)
-                diff = subtract_p(unit)
-                if unit + 1 < UNITS:
                     build_u(unit + 1, BOTTOM)
-                p_grouped = regroup_p(diff)
                 if unit > 0:
                     second_matmul(unit - 1)
                 a_bf = matmul_a(unit, 1)

@@ -5,6 +5,7 @@ from concourse.masks import make_identity
 
 BF16 = mybir.dt.bfloat16
 F32 = mybir.dt.float32
+I32 = mybir.dt.int32
 U32 = mybir.dt.uint32
 U8 = mybir.dt.uint8
 FP8X4 = mybir.dt.float8_e4m3fn_x4
@@ -24,10 +25,15 @@ COLS = ROW_TILES * P
 M_TILES = M // P
 UNITS = HALVES * KERNEL
 BANK = 512
-ROW_WORDS = WO // 2
 
-G_PLAIN, G_DOWN, G_LAST = 0, 1, 2
-TOP, BOTTOM = 0, 1
+SLOTS = 16
+RUN = WO // 2
+SLOT_WORDS = RUN // 2
+G_ROWS = HO + 2
+GM = M_TILES * P
+G_WORDS = GM + GM // 4
+
+G_DOWN, G_PLAIN, G_UP = 0, 1, 2
 
 
 def tile_convexrelucnn_t_kernel(tc, x, G, v, w, out):
@@ -40,12 +46,13 @@ def tile_convexrelucnn_t_kernel(tc, x, G, v, w, out):
         sums = pools.enter_context(tc.psum_pool(name="sums", bufs=1))
 
         x_sb = keep.tile([P, HALVES * ROW_TILES, H * W], BF16)
-        rows = keep.tile([P, UNITS, ROW_TILES, H * WO], BF16)
-        g_pad = keep.tile([P, M_TILES, WO + L], BF16)
-        g_last = keep.tile([P, M_TILES, L], BF16)
-        g_grouped = keep.tile([P, 3, M_TILES * P * 4], BF16, align_bytes=64)
-        g_codes = keep.tile([P, 3, M_TILES * P], U32, align_bytes=64)
-        g_scales = keep.tile([P, 3, M_TILES * P], U8, align_bytes=64)
+        rows = keep.tile([P, UNITS, 2, ROW_TILES, SLOTS * RUN], BF16)
+        edge_rows = keep.tile([P, HALVES, 2, ROW_TILES, SLOTS * RUN], BF16)
+        g_sb = keep.tile([P, M_TILES, L], BF16)
+        g_rows = keep.tile([P, M_TILES, 2, G_ROWS * RUN], BF16)
+        g_grouped = keep.tile([P, 3, GM * 4], BF16, align_bytes=64)
+        g_mx = keep.tile([P, 3, G_WORDS], U32, align_bytes=64)
+        edge_mx = keep.tile([P, 2, KERNEL, G_WORDS], U32, align_bytes=64)
         v_sb = keep.tile([P, M_TILES, K, O], BF16)
         w_sb = keep.tile([P, M_TILES, K, O], BF16)
         p_codes = keep.tile([P, M_TILES, KERNEL, KERNEL, O], U32, align_bytes=64)
@@ -58,17 +65,17 @@ def tile_convexrelucnn_t_kernel(tc, x, G, v, w, out):
         x_rows = x.rearrange("b c h w -> (b c) (h w)").rearrange(
             "(t p) f -> p t f", p=P
         )
-        nc.scalar.dma_start(
-            out=g_pad[:, :, WO:], in_=G.rearrange("(t p) n -> p t n", p=P)
-        )
-        for half in range(HALVES):
+
+        def zero_words(packed):
+            return packed.bitcast(U32)
+
+        def load_x(half):
             tiles = slice(half * ROW_TILES, (half + 1) * ROW_TILES)
             nc.sync.dma_start(out=x_sb[:, tiles, :], in_=x_rows[:, tiles, :])
-        for mt in range(M_TILES):
+
+        def load_p(mt):
             nc.sync.dma_start(out=v_sb[:, mt], in_=v[mt * P : (mt + 1) * P])
             nc.sync.dma_start(out=w_sb[:, mt], in_=w[mt * P : (mt + 1) * P])
-
-        make_identity(nc, ident[:])
 
         def flip_words(words):
             bank = banks.tile([P, BANK], F32, name="bank")
@@ -83,104 +90,112 @@ def tile_convexrelucnn_t_kernel(tc, x, G, v, w, out):
                 out=grouped_words, in_=blocks.rearrange("p r u c -> p r c u")
             )
 
-        def zero_g():
-            nc.vector.memset(g_pad[:, :, :WO], 0.0)
-            nc.vector.memset(g_last[:], 0.0)
-
-        def fill_g_last():
+        def pack_g():
             nc.vector.tensor_copy(
-                out=g_last[:, :, L - 2 * WO : L - WO], in_=g_pad[:, :, L : L + WO]
+                out=g_rows[:, :, :, RUN : (HO + 1) * RUN].rearrange(
+                    "p t u (h e) -> p t u h e", e=RUN
+                ),
+                in_=g_sb[:].rearrange("p t (h u e) -> p t u h e", u=2, e=RUN),
             )
 
-        def flip_g():
-            pad_words = g_pad[:].bitcast(F32)
-            last_words = g_last[:].bitcast(F32)
-            sources = {
-                G_PLAIN: (pad_words, ROW_WORDS),
-                G_DOWN: (pad_words, 0),
-                G_LAST: (last_words, 0),
-            }
-            for form in (G_PLAIN, G_DOWN, G_LAST):
-                source, start = sources[form]
-                blocks = flip_words(
-                    lambda mt, u: source[:, mt, start + u * P : start + (u + 1) * P]
-                )
-                leave_flip_bank(
-                    blocks,
-                    g_grouped[:, form, :]
-                    .bitcast(F32)
-                    .rearrange("p (r c u) -> p r c u", r=2, u=2),
-                )
+        def flip_g(form):
+            words = g_rows[:].rearrange("p t u f -> p (t u f)").bitcast(F32).rearrange(
+                "p (t u f) -> p t u f", t=M_TILES, u=2
+            )
+            start = form * SLOT_WORDS
+            blocks = flip_words(lambda mt, u: words[:, mt, u, start : start + P])
+            leave_flip_bank(
+                blocks,
+                g_grouped[:, form, :]
+                .bitcast(F32)
+                .rearrange("p (r c u) -> p r c u", r=2, u=2),
+            )
 
-        def quantise_g():
-            for form in (G_PLAIN, G_DOWN, G_LAST):
-                nc.vector.quantize_mx(
-                    out=g_codes[:, form, :].bitcast(FP8X4),
-                    scales=g_scales[:, form, :],
-                    in_=g_grouped[:, form, :],
-                )
+        def quantise_g(form):
+            nc.vector.quantize_mx(
+                out=g_mx[:, form, :GM].bitcast(FP8X4),
+                scales=g_mx[:, form, GM:].bitcast(U8),
+                in_=g_grouped[:, form, :],
+            )
 
-        u_mx = {}
+        def place_edge_g(j):
+            plain = g_mx[:, G_PLAIN, :].bitcast(I32)
+            first = edge_mx[:, 0, j, :].bitcast(I32)
+            last = edge_mx[:, 1, j, :].bitcast(I32)
+            q = 32 * j
+            nc.sync.dma_start(out=first[q : q + 8, :], in_=plain[0:8, :])
+            nc.sync.dma_start(out=last[q + 24 : q + 32, :GM], in_=plain[P - 8 : P, :GM])
+            nc.sync.dma_start(out=last[q : q + 4, GM:], in_=plain[96:100, GM:])
+
+        def row_runs(half, j, image_rows):
+            tiles = slice(half * ROW_TILES, (half + 1) * ROW_TILES)
+            return (
+                x_sb[:, tiles, :]
+                .rearrange("p t (h w) -> p t h w", w=W)[:, :, image_rows, j : j + WO]
+                .rearrange("p t h (u e) -> p u t h e", u=2)
+            )
 
         def pack_rows(unit):
             half, j = divmod(unit, KERNEL)
-            tiles = slice(half * ROW_TILES, (half + 1) * ROW_TILES)
             nc.vector.tensor_copy(
-                out=rows[:, unit].rearrange("p t (h w) -> p t h w", w=WO),
-                in_=x_sb[:, tiles, :].rearrange("p t (h w) -> p t h w", w=W)[
-                    :, :, :, j : j + WO
-                ],
+                out=rows[:, unit].rearrange("p u t (h e) -> p u t h e", e=RUN),
+                in_=row_runs(half, j, slice(1, HO + 1)),
             )
 
-        def build_u(unit, window):
-            row_words = rows[:, unit].bitcast(F32)
-            start = 2 * window * ROW_WORDS
+        def pack_edges(half):
+            slots = edge_rows[:, half].rearrange("p u t (h e) -> p u t h e", e=RUN)
+            for j in range(KERNEL):
+                nc.vector.tensor_copy(
+                    out=slots[:, :, :, 4 * j : 4 * j + 4 : 3, :],
+                    in_=row_runs(half, j, slice(0, H, H - 1)),
+                )
+
+        def flip_u(packed):
+            words = packed.rearrange("p u t f -> p (u t f)").bitcast(F32).rearrange(
+                "p (u t f) -> p u t f", u=2, t=ROW_TILES
+            )
             grouped = work.tile([P, COLS * 4], BF16, name="grouped", align_bytes=64)
             grouped_words = grouped[:].bitcast(F32).rearrange(
                 "p (t c u) -> p t c u", t=ROW_TILES, u=2
             )
             for pair in range(ROW_TILES // 2):
-                blocks = flip_words(
-                    lambda r, u: row_words[
-                        :, 2 * pair + r, start + u * P : start + (u + 1) * P
-                    ]
-                )
+                blocks = flip_words(lambda r, u: words[:, u, 2 * pair + r, :])
                 leave_flip_bank(blocks, grouped_words[:, 2 * pair : 2 * pair + 2, :, :])
-            codes = work.tile([P, COLS], U32, name="u_codes%d" % window, align_bytes=64)
-            scales = work.tile([P, COLS], U8, name="u_scales%d" % window, align_bytes=64)
+            return grouped
+
+        def quantise_u(grouped, name):
+            codes = work.tile([P, COLS], U32, name=name + "_codes", align_bytes=64)
+            scales = work.tile([P, COLS], U8, name=name + "_scales", align_bytes=64)
             nc.vector.quantize_mx(
                 out=codes[:].bitcast(FP8X4), scales=scales[:], in_=grouped[:]
             )
-            u_mx[(unit, window)] = (codes, scales)
+            return codes, scales
 
-        def first_pass(bank, form, mt, unit, window, start, stop):
-            codes, scales = u_mx[(unit, window)]
-            m_cols = slice(mt * P, (mt + 1) * P)
+        def first_pass(bank, g, mt, u_mx, start, stop):
+            codes, scales = u_mx
             nc.tensor.matmul_mx(
                 out=bank[:],
-                lhsT=g_codes[:, form, m_cols].bitcast(FP8X4),
-                lhsT_scale=g_scales[:, form, m_cols],
+                lhsT=g[:, mt * P : (mt + 1) * P].bitcast(FP8X4),
+                lhsT_scale=g[:, GM + mt * (P // 4) : GM + (mt + 1) * (P // 4)].bitcast(U8),
                 rhs=codes[:].bitcast(FP8X4),
                 rhs_scale=scales[:],
                 start=start,
                 stop=stop,
             )
 
-        def matmul_a(unit, i):
+        def matmul_a(i, j, middle, edges):
             a_bf = work.tile([P, M_TILES, COLS], BF16, name="a_bf", bufs=4, align_bytes=64)
             for mt in range(M_TILES):
                 bank = banks.tile([P, BANK], F32, name="bank")
-                if i == 0:
-                    first_pass(bank, G_PLAIN, mt, unit, TOP, True, True)
-                elif i == 1:
-                    first_pass(bank, G_DOWN, mt, unit, TOP, True, False)
-                    first_pass(bank, G_LAST, mt, unit, BOTTOM, False, True)
+                if i == 1:
+                    first_pass(bank, g_mx[:, G_PLAIN, :], mt, middle, True, True)
+                elif i == 0:
+                    first_pass(bank, g_mx[:, G_UP, :], mt, middle, True, False)
+                    first_pass(bank, edge_mx[:, 0, j, :], mt, edges, False, True)
                 else:
-                    first_pass(bank, G_PLAIN, mt, unit, BOTTOM, True, True)
-                if KERNEL <= unit < UNITS - 1 and i == 1 and mt == 1:
-                    nc.vector.tensor_copy(out=a_bf[:, mt, :], in_=bank[:])
-                else:
-                    nc.scalar.copy(out=a_bf[:, mt, :], in_=bank[:])
+                    first_pass(bank, g_mx[:, G_DOWN, :], mt, middle, True, False)
+                    first_pass(bank, edge_mx[:, 1, j, :], mt, edges, False, True)
+                nc.scalar.copy(out=a_bf[:, mt, :], in_=bank[:])
             return a_bf
 
         def quantise_a(unit, i, a_bf):
@@ -237,9 +252,9 @@ def tile_convexrelucnn_t_kernel(tc, x, G, v, w, out):
 
         def second_matmul(unit):
             half, j = divmod(unit, KERNEL)
-            for i in range(KERNEL):
-                opens = j == 0 and i == 0
-                closes = j == KERNEL - 1 and i == KERNEL - 1
+            for i in (1, 0, 2):
+                opens = j == 0 and i == 1
+                closes = j == KERNEL - 1 and i == 2
                 if half == 0:
                     second_pass(0, j, i, 0, opens, False)
                 else:
@@ -248,33 +263,65 @@ def tile_convexrelucnn_t_kernel(tc, x, G, v, w, out):
                     second_pass(1, j, i, 1, False, closes)
 
         with tc.manual_schedule():
-            zero_g()
-            fill_g_last()
-            flip_g()
+            nc.sync.dma_start(out=g_sb[:], in_=G.rearrange("(t p) n -> p t n", p=P))
+            load_x(0)
+            load_p(0)
+            make_identity(nc, ident[:])
+            nc.vector.memset(zero_words(g_rows[:].rearrange("p t u f -> p (t u f)")), 0)
+            nc.vector.memset(zero_words(edge_rows[:, 0].rearrange("p u t f -> p (u t f)")), 0)
+            nc.gpsimd.memset(g_mx[:, G_PLAIN, GM:], 0)
+            for j in range(KERNEL):
+                nc.gpsimd.memset(edge_mx[:, :, j, :], 0)
+            nc.gpsimd.memset(zero_words(edge_rows[:, 1].rearrange("p u t f -> p (u t f)")), 0)
+
+            pack_g()
+            flip_g(G_PLAIN)
+            flip_g(G_UP)
             pack_rows(0)
-            quantise_g()
+            quantise_g(G_PLAIN)
+            for j in range(KERNEL):
+                place_edge_g(j)
+            load_x(1)
+            load_p(1)
+            flip_g(G_DOWN)
+            grouped = flip_u(rows[:, 0])
+            quantise_g(G_UP)
+            pack_edges(0)
+            middle = quantise_u(grouped, "middle")
+            quantise_g(G_DOWN)
+            grouped = flip_u(edge_rows[:, 0])
             pack_rows(1)
-            build_u(0, TOP)
-            build_u(0, BOTTOM)
+            edges = quantise_u(grouped, "edges")
             pack_rows(2)
 
             for unit in range(UNITS):
-                if unit + KERNEL < UNITS:
-                    pack_rows(unit + KERNEL)
+                half, j = divmod(unit, KERNEL)
                 diff = subtract_p(unit)
-                a_bf = matmul_a(unit, 0)
-                quantise_a(unit, 0, a_bf)
+                if unit == KERNEL - 2:
+                    pack_edges(1)
+                a_bf = matmul_a(1, j, middle, edges)
+                quantise_a(unit, 1, a_bf)
+                if unit == KERNEL - 1:
+                    next_edges = quantise_u(grouped, "edges")
                 p_grouped = regroup_p(diff)
+                next_middle = None
                 if unit + 1 < UNITS:
-                    build_u(unit + 1, TOP)
-                    build_u(unit + 1, BOTTOM)
+                    grouped = flip_u(rows[:, unit + 1])
+                    next_middle = quantise_u(grouped, "middle")
                 if unit > 0:
                     second_matmul(unit - 1)
-                a_bf = matmul_a(unit, 1)
+                a_bf = matmul_a(0, j, middle, edges)
                 quantise_p(unit, p_grouped)
-                quantise_a(unit, 1, a_bf)
-                a_bf = matmul_a(unit, 2)
+                quantise_a(unit, 0, a_bf)
+                if unit + KERNEL < UNITS:
+                    pack_rows(unit + KERNEL)
+                a_bf = matmul_a(2, j, middle, edges)
                 quantise_a(unit, 2, a_bf)
+                if unit == KERNEL - 2:
+                    grouped = flip_u(edge_rows[:, 1])
+                middle = next_middle
+                if unit == KERNEL - 1:
+                    edges = next_edges
             second_matmul(UNITS - 1)
 
             result0 = work.tile([P, O], F32, name="result0")
@@ -282,4 +329,4 @@ def tile_convexrelucnn_t_kernel(tc, x, G, v, w, out):
             nc.scalar.copy(out=result0[:], in_=acc[0][:])
             nc.vector.tensor_copy(out=result1[:], in_=acc[1][:])
             nc.sync.dma_start(out=out[:P, :], in_=result0[:])
-            nc.sync.dma_start(out=out[P:, :], in_=result1[:])
+            nc.scalar.dma_start(out=out[P:, :], in_=result1[:])

@@ -47,12 +47,12 @@ def tile_convexrelucnn_t_kernel(tc, x, G, v, w, out):
 
         x_sb = keep.tile([P, HALVES * ROW_TILES, H * W], BF16)
         rows = keep.tile([P, UNITS, 2, ROW_TILES, SLOTS * RUN], BF16)
-        edge_rows = keep.tile([P, HALVES, 2, ROW_TILES, SLOTS * RUN], BF16)
+        edge_rows = keep.tile([P, 2, ROW_TILES, SLOTS * RUN], BF16)
         g_sb = keep.tile([P, M_TILES, L], BF16)
         g_rows = keep.tile([P, M_TILES, 2, G_ROWS * RUN], BF16)
         g_grouped = keep.tile([P, 3, GM * 4], BF16, align_bytes=64)
         g_mx = keep.tile([P, 3, G_WORDS], U32, align_bytes=64)
-        edge_mx = keep.tile([P, 2, KERNEL, G_WORDS], U32, align_bytes=64)
+        edge_mx = keep.tile([P, HALVES, 2, KERNEL, G_WORDS], U32, align_bytes=64)
         v_sb = keep.tile([P, M_TILES, K, O], BF16)
         w_sb = keep.tile([P, M_TILES, K, O], BF16)
         p_codes = keep.tile([P, M_TILES, KERNEL, KERNEL, O], U32, align_bytes=64)
@@ -73,9 +73,9 @@ def tile_convexrelucnn_t_kernel(tc, x, G, v, w, out):
             tiles = slice(half * ROW_TILES, (half + 1) * ROW_TILES)
             nc.sync.dma_start(out=x_sb[:, tiles, :], in_=x_rows[:, tiles, :])
 
-        def load_p(mt):
-            nc.sync.dma_start(out=v_sb[:, mt], in_=v[mt * P : (mt + 1) * P])
-            nc.sync.dma_start(out=w_sb[:, mt], in_=w[mt * P : (mt + 1) * P])
+        def load_p(queue, mt):
+            queue.dma_start(out=v_sb[:, mt], in_=v[mt * P : (mt + 1) * P])
+            queue.dma_start(out=w_sb[:, mt], in_=w[mt * P : (mt + 1) * P])
 
         def flip_words(words):
             bank = banks.tile([P, BANK], F32, name="bank")
@@ -111,6 +111,9 @@ def tile_convexrelucnn_t_kernel(tc, x, G, v, w, out):
                 .rearrange("p (r c u) -> p r c u", r=2, u=2),
             )
 
+        def edge_slots(half, j):
+            return (4 * j, 4 * j + 3) if half == 0 else (4 * j + 1, 4 * j + 2)
+
         def quantise_g(form):
             nc.vector.quantize_mx(
                 out=g_mx[:, form, :GM].bitcast(FP8X4),
@@ -118,14 +121,21 @@ def tile_convexrelucnn_t_kernel(tc, x, G, v, w, out):
                 in_=g_grouped[:, form, :],
             )
 
-        def place_edge_g(j):
+        def move_block(edge, slot, row):
             plain = g_mx[:, G_PLAIN, :].bitcast(I32)
-            first = edge_mx[:, 0, j, :].bitcast(I32)
-            last = edge_mx[:, 1, j, :].bitcast(I32)
-            q = 32 * j
-            nc.sync.dma_start(out=first[q : q + 8, :], in_=plain[0:8, :])
-            nc.sync.dma_start(out=last[q + 24 : q + 32, :GM], in_=plain[P - 8 : P, :GM])
-            nc.sync.dma_start(out=last[q : q + 4, GM:], in_=plain[96:100, GM:])
+            edge = edge.bitcast(I32)
+            to_scale, from_scale = 32 * (slot // 4) + slot % 4, 32 * (row // 4) + row % 4
+            nc.sync.dma_start(
+                out=edge[8 * slot : 8 * slot + 8, :GM], in_=plain[8 * row : 8 * row + 8, :GM]
+            )
+            nc.sync.dma_start(
+                out=edge[to_scale : to_scale + 1, GM:], in_=plain[from_scale : from_scale + 1, GM:]
+            )
+
+        def place_edge_g(half, j):
+            first_slot, last_slot = edge_slots(half, j)
+            move_block(edge_mx[:, half, 0, j, :], first_slot, 0)
+            move_block(edge_mx[:, half, 1, j, :], last_slot, HO - 1)
 
         def row_runs(half, j, image_rows):
             tiles = slice(half * ROW_TILES, (half + 1) * ROW_TILES)
@@ -137,16 +147,16 @@ def tile_convexrelucnn_t_kernel(tc, x, G, v, w, out):
 
         def pack_rows(unit):
             half, j = divmod(unit, KERNEL)
-            nc.vector.tensor_copy(
-                out=rows[:, unit].rearrange("p u t (h e) -> p u t h e", e=RUN),
-                in_=row_runs(half, j, slice(1, HO + 1)),
-            )
+            packed = rows[:, unit].rearrange("p u t (h e) -> p u t h e", e=RUN)
+            runs = row_runs(half, j, slice(1, HO + 1))
+            nc.vector.tensor_copy(out=packed, in_=runs)
 
         def pack_edges(half):
-            slots = edge_rows[:, half].rearrange("p u t (h e) -> p u t h e", e=RUN)
+            slots = edge_rows[:].rearrange("p u t (h e) -> p u t h e", e=RUN)
             for j in range(KERNEL):
+                first_slot, last_slot = edge_slots(half, j)
                 nc.vector.tensor_copy(
-                    out=slots[:, :, :, 4 * j : 4 * j + 4 : 3, :],
+                    out=slots[:, :, :, first_slot : last_slot + 1 : last_slot - first_slot, :],
                     in_=row_runs(half, j, slice(0, H, H - 1)),
                 )
 
@@ -164,8 +174,8 @@ def tile_convexrelucnn_t_kernel(tc, x, G, v, w, out):
             return grouped
 
         def quantise_u(grouped, name):
-            codes = work.tile([P, COLS], U32, name=name + "_codes", align_bytes=64)
-            scales = work.tile([P, COLS], U8, name=name + "_scales", align_bytes=64)
+            codes = work.tile([P, COLS], U32, name=name + "_codes", bufs=4, align_bytes=64)
+            scales = work.tile([P, COLS], U8, name=name + "_scales", bufs=4, align_bytes=64)
             nc.vector.quantize_mx(
                 out=codes[:].bitcast(FP8X4), scales=scales[:], in_=grouped[:]
             )
@@ -183,19 +193,23 @@ def tile_convexrelucnn_t_kernel(tc, x, G, v, w, out):
                 stop=stop,
             )
 
-        def matmul_a(i, j, middle, edges):
+        def matmul_a(unit, i, middle, edges):
+            half, j = divmod(unit, KERNEL)
             a_bf = work.tile([P, M_TILES, COLS], BF16, name="a_bf", bufs=4, align_bytes=64)
             for mt in range(M_TILES):
                 bank = banks.tile([P, BANK], F32, name="bank")
                 if i == 1:
-                    first_pass(bank, g_mx[:, G_PLAIN, :], mt, middle, True, True)
+                    first_pass(bank, g_mx[:, G_PLAIN, :], mt, middle[unit], True, True)
                 elif i == 0:
-                    first_pass(bank, g_mx[:, G_UP, :], mt, middle, True, False)
-                    first_pass(bank, edge_mx[:, 0, j, :], mt, edges, False, True)
+                    first_pass(bank, g_mx[:, G_UP, :], mt, middle[unit], True, False)
+                    first_pass(bank, edge_mx[:, half, 0, j, :], mt, edges, False, True)
                 else:
-                    first_pass(bank, g_mx[:, G_DOWN, :], mt, middle, True, False)
-                    first_pass(bank, edge_mx[:, 1, j, :], mt, edges, False, True)
-                nc.scalar.copy(out=a_bf[:, mt, :], in_=bank[:])
+                    first_pass(bank, g_mx[:, G_DOWN, :], mt, middle[unit], True, False)
+                    first_pass(bank, edge_mx[:, half, 1, j, :], mt, edges, False, True)
+                if unit == UNITS - 1 and i == 2 and mt == 1:
+                    nc.vector.tensor_copy(out=a_bf[:, mt, :], in_=bank[:])
+                else:
+                    nc.scalar.copy(out=a_bf[:, mt, :], in_=bank[:])
             return a_bf
 
         def quantise_a(unit, i, a_bf):
@@ -231,11 +245,11 @@ def tile_convexrelucnn_t_kernel(tc, x, G, v, w, out):
 
         def quantise_p(unit, p_grouped):
             mt, j = divmod(unit, KERNEL)
-            for i in range(KERNEL):
+            for i in (slice(0, 2), slice(2, 3)):
                 nc.vector.quantize_mx(
-                    out=p_codes[:, mt, j, i, :].bitcast(FP8X4),
-                    scales=p_scales[:, mt, j, i, :],
-                    in_=p_grouped[:, i].rearrange("p o c -> p (o c)"),
+                    out=p_codes[:, mt, j, i, :].rearrange("p i o -> p (i o)").bitcast(FP8X4),
+                    scales=p_scales[:, mt, j, i, :].rearrange("p i o -> p (i o)"),
+                    in_=p_grouped[:, i].rearrange("p i o c -> p (i o c)"),
                 )
 
         def second_pass(half, j, i, mt, start, stop):
@@ -263,65 +277,84 @@ def tile_convexrelucnn_t_kernel(tc, x, G, v, w, out):
                     second_pass(1, j, i, 1, False, closes)
 
         with tc.manual_schedule():
-            nc.sync.dma_start(out=g_sb[:], in_=G.rearrange("(t p) n -> p t n", p=P))
             load_x(0)
-            load_p(0)
+            nc.sync.dma_start(out=g_sb[:], in_=G.rearrange("(t p) n -> p t n", p=P))
+            load_p(nc.sync, 0)
+            load_x(1)
             make_identity(nc, ident[:])
             nc.vector.memset(zero_words(g_rows[:].rearrange("p t u f -> p (t u f)")), 0)
-            nc.vector.memset(zero_words(edge_rows[:, 0].rearrange("p u t f -> p (u t f)")), 0)
-            nc.gpsimd.memset(g_mx[:, G_PLAIN, GM:], 0)
-            for j in range(KERNEL):
-                nc.gpsimd.memset(edge_mx[:, :, j, :], 0)
-            nc.gpsimd.memset(zero_words(edge_rows[:, 1].rearrange("p u t f -> p (u t f)")), 0)
+            nc.vector.memset(zero_words(edge_rows[:].rearrange("p u t f -> p (u t f)")), 0)
+            nc.gpsimd.memset(edge_mx[:, 0].rearrange("p e j f -> p (e j f)"), 0)
+            nc.gpsimd.memset(edge_mx[:, 1].rearrange("p e j f -> p (e j f)"), 0)
 
+            middle, diff, p_grouped = {}, {}, {}
+
+            def flip_middle(unit):
+                middle[unit] = flip_u(rows[:, unit])
+
+            def quantise_middle(unit):
+                middle[unit] = quantise_u(middle[unit], "middle")
+
+            pack_rows(0)
+            flip_middle(0)
             pack_g()
             flip_g(G_PLAIN)
-            flip_g(G_UP)
-            pack_rows(0)
-            quantise_g(G_PLAIN)
-            for j in range(KERNEL):
-                place_edge_g(j)
-            load_x(1)
-            load_p(1)
-            flip_g(G_DOWN)
-            grouped = flip_u(rows[:, 0])
-            quantise_g(G_UP)
-            pack_edges(0)
-            middle = quantise_u(grouped, "middle")
-            quantise_g(G_DOWN)
-            grouped = flip_u(edge_rows[:, 0])
             pack_rows(1)
-            edges = quantise_u(grouped, "edges")
+            flip_middle(1)
             pack_rows(2)
+            pack_edges(0)
+            quantise_middle(0)
+            quantise_g(G_PLAIN)
+            for half in range(HALVES):
+                for j in range(KERNEL):
+                    place_edge_g(half, j)
+            load_p(nc.sync, 1)
+            a_bf = {}
+            a_bf[0] = matmul_a(0, 1, middle, None)
+            quantise_middle(1)
+            flip_middle(2)
+            diff[0] = subtract_p(0)
+            a_bf[1] = matmul_a(1, 1, middle, None)
+            quantise_a(0, 1, a_bf[0])
+            pack_edges(1)
+            flip_g(G_UP)
+            flip_g(G_DOWN)
+            quantise_middle(2)
+            edge_grouped = flip_u(edge_rows[:])
+            p_grouped[0] = regroup_p(diff[0])
+            quantise_a(1, 1, a_bf[1])
+            a_bf[2] = matmul_a(2, 1, middle, None)
+            quantise_g(G_UP)
+            quantise_g(G_DOWN)
+            pack_rows(3)
+            edges = quantise_u(edge_grouped, "edges")
+            diff[1] = subtract_p(1)
+            quantise_a(2, 1, a_bf[2])
+            quantise_p(0, p_grouped[0])
 
             for unit in range(UNITS):
-                half, j = divmod(unit, KERNEL)
-                diff = subtract_p(unit)
-                if unit == KERNEL - 2:
-                    pack_edges(1)
-                a_bf = matmul_a(1, j, middle, edges)
-                quantise_a(unit, 1, a_bf)
-                if unit == KERNEL - 1:
-                    next_edges = quantise_u(grouped, "edges")
-                p_grouped = regroup_p(diff)
-                next_middle = None
+                ahead = unit + KERNEL
+                if ahead < UNITS:
+                    flip_middle(ahead)
                 if unit + 1 < UNITS:
-                    grouped = flip_u(rows[:, unit + 1])
-                    next_middle = quantise_u(grouped, "middle")
+                    p_grouped[unit + 1] = regroup_p(diff[unit + 1])
+                a_bf[0] = matmul_a(unit, 0, middle, edges)
+                if ahead < UNITS:
+                    quantise_middle(ahead)
+                if unit + 2 < UNITS:
+                    diff[unit + 2] = subtract_p(unit + 2)
+                quantise_a(unit, 0, a_bf[0])
+                if ahead + 1 < UNITS:
+                    pack_rows(ahead + 1)
+                if unit + 1 < UNITS:
+                    quantise_p(unit + 1, p_grouped[unit + 1])
+                a_bf[2] = matmul_a(unit, 2, middle, edges)
+                quantise_a(unit, 2, a_bf[2])
+                if ahead < UNITS:
+                    a_bf[1] = matmul_a(ahead, 1, middle, None)
+                    quantise_a(ahead, 1, a_bf[1])
                 if unit > 0:
                     second_matmul(unit - 1)
-                a_bf = matmul_a(0, j, middle, edges)
-                quantise_p(unit, p_grouped)
-                quantise_a(unit, 0, a_bf)
-                if unit + KERNEL < UNITS:
-                    pack_rows(unit + KERNEL)
-                a_bf = matmul_a(2, j, middle, edges)
-                quantise_a(unit, 2, a_bf)
-                if unit == KERNEL - 2:
-                    grouped = flip_u(edge_rows[:, 1])
-                middle = next_middle
-                if unit == KERNEL - 1:
-                    edges = next_edges
             second_matmul(UNITS - 1)
 
             result0 = work.tile([P, O], F32, name="result0")

@@ -23,6 +23,7 @@ HALVES = 2
 ROW_TILES = 4
 COLS = ROW_TILES * P
 M_TILES = M // P
+X_PITCH = 624
 UNITS = HALVES * KERNEL
 BANK = 512
 
@@ -30,6 +31,7 @@ SLOTS = 16
 RUN = WO // 2
 SLOT_WORDS = RUN // 2
 G_ROWS = HO + 2
+KERNEL_SLOTS = 2 * HALVES
 GM = M_TILES * P
 G_WORDS = GM + GM // 4
 
@@ -45,14 +47,15 @@ def tile_convexrelucnn_t_kernel(tc, x, G, v, w, out):
         banks = pools.enter_context(tc.psum_pool(name="banks", bufs=6))
         sums = pools.enter_context(tc.psum_pool(name="sums", bufs=1))
 
-        x_sb = keep.tile([P, HALVES * ROW_TILES, H * W], BF16)
+        x_sb = keep.tile([P, HALVES * ROW_TILES, X_PITCH], BF16)
         rows = keep.tile([P, UNITS, 2, ROW_TILES, SLOTS * RUN], BF16)
         edge_rows = keep.tile([P, 2, ROW_TILES, SLOTS * RUN], BF16)
         g_sb = keep.tile([P, M_TILES, L], BF16)
         g_rows = keep.tile([P, M_TILES, 2, G_ROWS * RUN], BF16)
         g_grouped = keep.tile([P, 3, GM * 4], BF16, align_bytes=64)
         g_mx = keep.tile([P, 3, G_WORDS], U32, align_bytes=64)
-        edge_mx = keep.tile([P, HALVES, 2, KERNEL, G_WORDS], U32, align_bytes=64)
+        edge_codes = keep.tile([P, HALVES, 2, KERNEL, GM], U32, align_bytes=64)
+        edge_scales = keep.tile([P, HALVES, GM], U8, align_bytes=64)
         v_sb = keep.tile([P, M_TILES, K, O], BF16)
         w_sb = keep.tile([P, M_TILES, K, O], BF16)
         p_codes = keep.tile([P, M_TILES, KERNEL, KERNEL, O], U32, align_bytes=64)
@@ -66,12 +69,10 @@ def tile_convexrelucnn_t_kernel(tc, x, G, v, w, out):
             "(t p) f -> p t f", p=P
         )
 
-        def zero_words(packed):
-            return packed.bitcast(U32)
 
-        def load_x(half):
-            tiles = slice(half * ROW_TILES, (half + 1) * ROW_TILES)
-            nc.sync.dma_start(out=x_sb[:, tiles, :], in_=x_rows[:, tiles, :])
+        def load_x(first, count):
+            tiles = slice(first, first + count)
+            nc.sync.dma_start(out=x_sb[:, tiles, : H * W], in_=x_rows[:, tiles, :])
 
         def load_p(queue, mt):
             queue.dma_start(out=v_sb[:, mt], in_=v[mt * P : (mt + 1) * P])
@@ -111,8 +112,8 @@ def tile_convexrelucnn_t_kernel(tc, x, G, v, w, out):
                 .rearrange("p (r c u) -> p r c u", r=2, u=2),
             )
 
-        def edge_slots(half, j):
-            return (4 * j, 4 * j + 3) if half == 0 else (4 * j + 1, 4 * j + 2)
+        def edge_slot(half, edge, j):
+            return KERNEL_SLOTS * j + HALVES * edge + half
 
         def quantise_g(form):
             nc.vector.quantize_mx(
@@ -121,43 +122,46 @@ def tile_convexrelucnn_t_kernel(tc, x, G, v, w, out):
                 in_=g_grouped[:, form, :],
             )
 
-        def move_block(edge, slot, row):
-            plain = g_mx[:, G_PLAIN, :].bitcast(I32)
-            edge = edge.bitcast(I32)
+        def place_edge_g(half, edge, j):
+            slot, row = edge_slot(half, edge, j), (HO - 1) * edge
             to_scale, from_scale = 32 * (slot // 4) + slot % 4, 32 * (row // 4) + row % 4
             nc.sync.dma_start(
-                out=edge[8 * slot : 8 * slot + 8, :GM], in_=plain[8 * row : 8 * row + 8, :GM]
+                out=edge_codes[8 * slot : 8 * slot + 8, half, edge, j, :].bitcast(I32),
+                in_=g_mx[8 * row : 8 * row + 8, G_PLAIN, :GM].bitcast(I32),
             )
             nc.sync.dma_start(
-                out=edge[to_scale : to_scale + 1, GM:], in_=plain[from_scale : from_scale + 1, GM:]
+                out=edge_scales[to_scale : to_scale + 1, half, :].bitcast(I32),
+                in_=g_mx[from_scale : from_scale + 1, G_PLAIN, GM:].bitcast(I32),
             )
 
-        def place_edge_g(half, j):
-            first_slot, last_slot = edge_slots(half, j)
-            move_block(edge_mx[:, half, 0, j, :], first_slot, 0)
-            move_block(edge_mx[:, half, 1, j, :], last_slot, HO - 1)
-
-        def row_runs(half, j, image_rows):
-            tiles = slice(half * ROW_TILES, (half + 1) * ROW_TILES)
+        def row_runs(tiles, j, image_rows):
             return (
-                x_sb[:, tiles, :]
+                x_sb[:, tiles, : H * W]
                 .rearrange("p t (h w) -> p t h w", w=W)[:, :, image_rows, j : j + WO]
                 .rearrange("p t h (u e) -> p u t h e", u=2)
             )
 
-        def pack_rows(unit):
+        def pack_rows(unit, parts=1):
             half, j = divmod(unit, KERNEL)
-            packed = rows[:, unit].rearrange("p u t (h e) -> p u t h e", e=RUN)
-            runs = row_runs(half, j, slice(1, HO + 1))
-            nc.vector.tensor_copy(out=packed, in_=runs)
+            count = ROW_TILES // parts
+            for first in range(0, ROW_TILES, count):
+                tiles = slice(half * ROW_TILES + first, half * ROW_TILES + first + count)
+                nc.vector.tensor_copy(
+                    out=rows[:, unit, :, first : first + count].rearrange(
+                        "p u t (h e) -> p u t h e", e=RUN
+                    ),
+                    in_=row_runs(tiles, j, slice(1, HO + 1)),
+                )
 
         def pack_edges(half):
             slots = edge_rows[:].rearrange("p u t (h e) -> p u t h e", e=RUN)
             for j in range(KERNEL):
-                first_slot, last_slot = edge_slots(half, j)
+                first_slot, last_slot = edge_slot(half, 0, j), edge_slot(half, 1, j)
                 nc.vector.tensor_copy(
                     out=slots[:, :, :, first_slot : last_slot + 1 : last_slot - first_slot, :],
-                    in_=row_runs(half, j, slice(0, H, H - 1)),
+                    in_=row_runs(
+                        slice(half * ROW_TILES, (half + 1) * ROW_TILES), j, slice(0, H, H - 1)
+                    ),
                 )
 
         def flip_u(packed):
@@ -181,31 +185,41 @@ def tile_convexrelucnn_t_kernel(tc, x, G, v, w, out):
             )
             return codes, scales
 
-        def first_pass(bank, g, mt, u_mx, start, stop):
+        def first_pass(bank, g_codes, g_scales, mt, u_mx, start, stop):
             codes, scales = u_mx
+            m_cols = slice(mt * P, (mt + 1) * P)
             nc.tensor.matmul_mx(
                 out=bank[:],
-                lhsT=g[:, mt * P : (mt + 1) * P].bitcast(FP8X4),
-                lhsT_scale=g[:, GM + mt * (P // 4) : GM + (mt + 1) * (P // 4)].bitcast(U8),
+                lhsT=g_codes[:, m_cols].bitcast(FP8X4),
+                lhsT_scale=g_scales[:, m_cols],
                 rhs=codes[:].bitcast(FP8X4),
                 rhs_scale=scales[:],
                 start=start,
                 stop=stop,
             )
 
-        def matmul_a(unit, i, middle, edges):
+        def middle_pass(bank, form, mt, u_mx, stop):
+            g_scales = g_mx[:, form, GM:].bitcast(U8)
+            first_pass(bank, g_mx[:, form, :GM], g_scales, mt, u_mx, True, stop)
+
+        def edge_pass(bank, unit, edge, mt, u_mx):
             half, j = divmod(unit, KERNEL)
+            first_pass(
+                bank, edge_codes[:, half, edge, j, :], edge_scales[:, half, :], mt, u_mx, False, True
+            )
+
+        def matmul_a(unit, i, middle, edges):
             a_bf = work.tile([P, M_TILES, COLS], BF16, name="a_bf", bufs=4, align_bytes=64)
             for mt in range(M_TILES):
                 bank = banks.tile([P, BANK], F32, name="bank")
                 if i == 1:
-                    first_pass(bank, g_mx[:, G_PLAIN, :], mt, middle[unit], True, True)
+                    middle_pass(bank, G_PLAIN, mt, middle[unit], True)
                 elif i == 0:
-                    first_pass(bank, g_mx[:, G_UP, :], mt, middle[unit], True, False)
-                    first_pass(bank, edge_mx[:, half, 0, j, :], mt, edges, False, True)
+                    middle_pass(bank, G_UP, mt, middle[unit], False)
+                    edge_pass(bank, unit, 0, mt, edges)
                 else:
-                    first_pass(bank, g_mx[:, G_DOWN, :], mt, middle[unit], True, False)
-                    first_pass(bank, edge_mx[:, half, 1, j, :], mt, edges, False, True)
+                    middle_pass(bank, G_DOWN, mt, middle[unit], False)
+                    edge_pass(bank, unit, 1, mt, edges)
                 if unit == UNITS - 1 and i == 2 and mt == 1:
                     nc.vector.tensor_copy(out=a_bf[:, mt, :], in_=bank[:])
                 else:
@@ -277,15 +291,20 @@ def tile_convexrelucnn_t_kernel(tc, x, G, v, w, out):
                     second_pass(1, j, i, 1, False, closes)
 
         with tc.manual_schedule():
-            load_x(0)
+            load_x(0, 2)
+            load_x(2, 2)
             nc.sync.dma_start(out=g_sb[:], in_=G.rearrange("(t p) n -> p t n", p=P))
             load_p(nc.sync, 0)
-            load_x(1)
+            load_x(ROW_TILES, ROW_TILES)
             make_identity(nc, ident[:])
-            nc.vector.memset(zero_words(g_rows[:].rearrange("p t u f -> p (t u f)")), 0)
-            nc.vector.memset(zero_words(edge_rows[:].rearrange("p u t f -> p (u t f)")), 0)
-            nc.gpsimd.memset(edge_mx[:, 0].rearrange("p e j f -> p (e j f)"), 0)
-            nc.gpsimd.memset(edge_mx[:, 1].rearrange("p e j f -> p (e j f)"), 0)
+            nc.vector.memset(g_rows[:, :, :, :RUN].bitcast(U32), 0)
+            nc.vector.memset(g_rows[:, :, :, (HO + 1) * RUN :].bitcast(U32), 0)
+            nc.vector.memset(edge_rows[:, :, :, KERNEL * KERNEL_SLOTS * RUN :].bitcast(U32), 0)
+            nc.vector.memset(edge_scales[:].rearrange("p h m -> p (h m)").bitcast(U32), 0)
+            nc.vector.memset(edge_codes[:, 0].rearrange("p e j m -> p (e j m)"), 0)
+            for edge in range(2):
+                for j in range(KERNEL):
+                    nc.gpsimd.memset(edge_codes[:, 1, edge, j, :], 0)
 
             middle, diff, p_grouped = {}, {}, {}
 
@@ -295,7 +314,7 @@ def tile_convexrelucnn_t_kernel(tc, x, G, v, w, out):
             def quantise_middle(unit):
                 middle[unit] = quantise_u(middle[unit], "middle")
 
-            pack_rows(0)
+            pack_rows(0, parts=2)
             flip_middle(0)
             pack_g()
             flip_g(G_PLAIN)
@@ -305,14 +324,17 @@ def tile_convexrelucnn_t_kernel(tc, x, G, v, w, out):
             pack_edges(0)
             quantise_middle(0)
             quantise_g(G_PLAIN)
-            for half in range(HALVES):
-                for j in range(KERNEL):
-                    place_edge_g(half, j)
-            load_p(nc.sync, 1)
+            for j in range(KERNEL):
+                for edge in range(2):
+                    place_edge_g(0, edge, j)
             a_bf = {}
             a_bf[0] = matmul_a(0, 1, middle, None)
             quantise_middle(1)
             flip_middle(2)
+            for j in range(KERNEL):
+                for edge in range(2):
+                    place_edge_g(1, edge, j)
+            load_p(nc.sync, 1)
             diff[0] = subtract_p(0)
             a_bf[1] = matmul_a(1, 1, middle, None)
             quantise_a(0, 1, a_bf[0])

@@ -331,14 +331,15 @@ def tile_convexrelucnn_t_kernel(tc, x, G, v, w, out):
             a_bf[0] = matmul_a(0, 1, middle, None)
             quantise_middle(1)
             flip_middle(2)
+            load_p(nc.sync, 1)
             for j in range(KERNEL):
                 for edge in range(2):
                     place_edge_g(1, edge, j)
-            load_p(nc.sync, 1)
             diff[0] = subtract_p(0)
             a_bf[1] = matmul_a(1, 1, middle, None)
             quantise_a(0, 1, a_bf[0])
             pack_edges(1)
+            pack_rows(3)
             flip_g(G_UP)
             flip_g(G_DOWN)
             quantise_middle(2)
@@ -348,7 +349,6 @@ def tile_convexrelucnn_t_kernel(tc, x, G, v, w, out):
             a_bf[2] = matmul_a(2, 1, middle, None)
             quantise_g(G_UP)
             quantise_g(G_DOWN)
-            pack_rows(3)
             edges = quantise_u(edge_grouped, "edges")
             diff[1] = subtract_p(1)
             quantise_a(2, 1, a_bf[2])
@@ -363,11 +363,11 @@ def tile_convexrelucnn_t_kernel(tc, x, G, v, w, out):
                 a_bf[0] = matmul_a(unit, 0, middle, edges)
                 if ahead < UNITS:
                     quantise_middle(ahead)
+                if ahead + 1 < UNITS:
+                    pack_rows(ahead + 1)
                 if unit + 2 < UNITS:
                     diff[unit + 2] = subtract_p(unit + 2)
                 quantise_a(unit, 0, a_bf[0])
-                if ahead + 1 < UNITS:
-                    pack_rows(ahead + 1)
                 if unit + 1 < UNITS:
                     quantise_p(unit + 1, p_grouped[unit + 1])
                 a_bf[2] = matmul_a(unit, 2, middle, edges)
@@ -375,8 +375,9 @@ def tile_convexrelucnn_t_kernel(tc, x, G, v, w, out):
                 if ahead < UNITS:
                     a_bf[1] = matmul_a(ahead, 1, middle, None)
                     quantise_a(ahead, 1, a_bf[1])
-                if unit > 0:
-                    second_matmul(unit - 1)
+                if unit > 1:
+                    second_matmul(unit - 2)
+            second_matmul(UNITS - 2)
             second_matmul(UNITS - 1)
 
             result0 = work.tile([P, O], F32, name="result0")

@@ -35,6 +35,8 @@ KERNEL_SLOTS = 2 * HALVES
 GM = M_TILES * P
 G_WORDS = GM + GM // 4
 
+ORDER = (0, 1, 3, 4, 2, 5)
+
 G_DOWN, G_PLAIN, G_UP = 0, 1, 2
 
 
@@ -55,7 +57,7 @@ def tile_convexrelucnn_t_kernel(tc, x, G, v, w, out):
         g_grouped = keep.tile([P, 3, GM * 4], BF16, align_bytes=64)
         g_mx = keep.tile([P, 3, G_WORDS], U32, align_bytes=64)
         edge_codes = keep.tile([P, HALVES, 2, KERNEL, GM], U32, align_bytes=64)
-        edge_scales = keep.tile([P, HALVES, GM], U8, align_bytes=64)
+        edge_scales = keep.tile([P, HALVES, KERNEL, GM], U8, align_bytes=64)
         v_sb = keep.tile([P, M_TILES, K, O], BF16)
         w_sb = keep.tile([P, M_TILES, K, O], BF16)
         p_codes = keep.tile([P, M_TILES, KERNEL, KERNEL, O], U32, align_bytes=64)
@@ -130,7 +132,7 @@ def tile_convexrelucnn_t_kernel(tc, x, G, v, w, out):
                 in_=g_mx[8 * row : 8 * row + 8, G_PLAIN, :GM].bitcast(I32),
             )
             nc.sync.dma_start(
-                out=edge_scales[to_scale : to_scale + 1, half, :].bitcast(I32),
+                out=edge_scales[to_scale : to_scale + 1, half, j, :].bitcast(I32),
                 in_=g_mx[from_scale : from_scale + 1, G_PLAIN, GM:].bitcast(I32),
             )
 
@@ -164,11 +166,14 @@ def tile_convexrelucnn_t_kernel(tc, x, G, v, w, out):
                     ),
                 )
 
+        def new_grouped():
+            return work.tile([P, COLS * 4], BF16, name="grouped", bufs=7, align_bytes=64)
+
         def flip_u(packed):
             words = packed.rearrange("p u t f -> p (u t f)").bitcast(F32).rearrange(
                 "p (u t f) -> p u t f", u=2, t=ROW_TILES
             )
-            grouped = work.tile([P, COLS * 4], BF16, name="grouped", align_bytes=64)
+            grouped = new_grouped()
             grouped_words = grouped[:].bitcast(F32).rearrange(
                 "p (t c u) -> p t c u", t=ROW_TILES, u=2
             )
@@ -177,9 +182,40 @@ def tile_convexrelucnn_t_kernel(tc, x, G, v, w, out):
                 leave_flip_bank(blocks, grouped_words[:, 2 * pair : 2 * pair + 2, :, :])
             return grouped
 
+        def pack_row_ends(half):
+            first = (KERNEL * KERNEL_SLOTS + 2 * half) * SLOT_WORDS
+            x_words = x_sb[:, half * ROW_TILES : (half + 1) * ROW_TILES, : H * W].bitcast(F32)
+            nc.vector.tensor_copy(
+                out=edge_rows[:]
+                .rearrange("p u t f -> p (u t f)")
+                .bitcast(F32)
+                .rearrange("p (u t f) -> p u t f", u=2, t=ROW_TILES)[
+                    :, :, :, first : first + HO
+                ],
+                in_=x_words.rearrange("p t (h w) -> p t h w", w=W // 2)[
+                    :, :, 1 : HO + 1, SLOT_WORDS :: SLOT_WORDS
+                ].rearrange("p t h u -> p u t h"),
+            )
+
+        def shift_words(source):
+            shifted = new_grouped()
+            for low, high in ((0, P // 2), (P // 2, P - 1)):
+                nc.sync.dma_start(
+                    out=shifted[low:high, :].bitcast(I32),
+                    in_=source[low + 1 : high + 1, :].bitcast(I32),
+                )
+            return shifted
+
+        def place_row_ends(half, shifted, ends):
+            first = SLOT_WORDS * (KERNEL * KERNEL_SLOTS + 2 * half)
+            nc.sync.dma_start(
+                out=shifted[SLOT_WORDS - 1 :: SLOT_WORDS, :].bitcast(I32),
+                in_=ends[first : first + HO, :].bitcast(I32),
+            )
+
         def quantise_u(grouped, name):
-            codes = work.tile([P, COLS], U32, name=name + "_codes", bufs=4, align_bytes=64)
-            scales = work.tile([P, COLS], U8, name=name + "_scales", bufs=4, align_bytes=64)
+            codes = work.tile([P, COLS], U32, name=name + "_codes", bufs=UNITS, align_bytes=64)
+            scales = work.tile([P, COLS], U8, name=name + "_scales", bufs=UNITS, align_bytes=64)
             nc.vector.quantize_mx(
                 out=codes[:].bitcast(FP8X4), scales=scales[:], in_=grouped[:]
             )
@@ -205,7 +241,7 @@ def tile_convexrelucnn_t_kernel(tc, x, G, v, w, out):
         def edge_pass(bank, unit, edge, mt, u_mx):
             half, j = divmod(unit, KERNEL)
             first_pass(
-                bank, edge_codes[:, half, edge, j, :], edge_scales[:, half, :], mt, u_mx, False, True
+                bank, edge_codes[:, half, edge, j, :], edge_scales[:, half, j, :], mt, u_mx, False, True
             )
 
         def matmul_a(unit, i, middle, edges):
@@ -220,7 +256,7 @@ def tile_convexrelucnn_t_kernel(tc, x, G, v, w, out):
                 else:
                     middle_pass(bank, G_DOWN, mt, middle[unit], False)
                     edge_pass(bank, unit, 1, mt, edges)
-                if unit == UNITS - 1 and i == 2 and mt == 1:
+                if False:
                     nc.vector.tensor_copy(out=a_bf[:, mt, :], in_=bank[:])
                 else:
                     nc.scalar.copy(out=a_bf[:, mt, :], in_=bank[:])
@@ -278,41 +314,46 @@ def tile_convexrelucnn_t_kernel(tc, x, G, v, w, out):
                 stop=stop,
             )
 
-        def second_matmul(unit):
-            half, j = divmod(unit, KERNEL)
-            for i in (1, 0, 2):
-                opens = j == 0 and i == 1
-                closes = j == KERNEL - 1 and i == 2
-                if half == 0:
-                    second_pass(0, j, i, 0, opens, False)
-                else:
-                    second_pass(0, j, i, 1, False, closes)
-                    second_pass(1, j, i, 0, opens, False)
-                    second_pass(1, j, i, 1, False, closes)
+        passes_done = [0, 0]
+
+        def second_matmul(step):
+            for half in range(HALVES):
+                for mt in range(M_TILES):
+                    for j in range(KERNEL):
+                        if max(ORDER.index(half * KERNEL + j), mt * KERNEL + j) == step:
+                            for i in range(KERNEL):
+                                passes_done[half] += 1
+                                second_pass(
+                                    half,
+                                    j,
+                                    i,
+                                    mt,
+                                    passes_done[half] == 1,
+                                    passes_done[half] == M_TILES * KERNEL * KERNEL,
+                                )
 
         with tc.manual_schedule():
             load_x(0, 2)
             load_x(2, 2)
             nc.sync.dma_start(out=g_sb[:], in_=G.rearrange("(t p) n -> p t n", p=P))
-            load_p(nc.sync, 0)
             load_x(ROW_TILES, ROW_TILES)
+            load_p(nc.sync, 0)
             make_identity(nc, ident[:])
             nc.vector.memset(g_rows[:, :, :, :RUN].bitcast(U32), 0)
             nc.vector.memset(g_rows[:, :, :, (HO + 1) * RUN :].bitcast(U32), 0)
-            nc.vector.memset(edge_rows[:, :, :, KERNEL * KERNEL_SLOTS * RUN :].bitcast(U32), 0)
-            nc.vector.memset(edge_scales[:].rearrange("p h m -> p (h m)").bitcast(U32), 0)
+            nc.vector.memset(edge_scales[:].rearrange("p h j m -> p (h j m)").bitcast(U32), 0)
             nc.vector.memset(edge_codes[:, 0].rearrange("p e j m -> p (e j m)"), 0)
             for edge in range(2):
                 for j in range(KERNEL):
                     nc.gpsimd.memset(edge_codes[:, 1, edge, j, :], 0)
 
-            middle, diff, p_grouped = {}, {}, {}
+            grouped, middle, diff, p_grouped = {}, {}, {}, {}
 
             def flip_middle(unit):
-                middle[unit] = flip_u(rows[:, unit])
+                grouped[unit] = flip_u(rows[:, unit])
 
             def quantise_middle(unit):
-                middle[unit] = quantise_u(middle[unit], "middle")
+                middle[unit] = quantise_u(grouped[unit], "middle")
 
             pack_rows(0, parts=2)
             flip_middle(0)
@@ -320,63 +361,72 @@ def tile_convexrelucnn_t_kernel(tc, x, G, v, w, out):
             flip_g(G_PLAIN)
             pack_rows(1)
             flip_middle(1)
-            pack_rows(2)
-            pack_edges(0)
+            for half in range(HALVES):
+                pack_edges(half)
+                pack_row_ends(half)
+            ends = flip_u(edge_rows[:])
             quantise_middle(0)
             quantise_g(G_PLAIN)
-            for j in range(KERNEL):
-                for edge in range(2):
-                    place_edge_g(0, edge, j)
+            for edge in range(2):
+                place_edge_g(0, edge, 0)
+            grouped[2] = shift_words(grouped[0])
             a_bf = {}
             a_bf[0] = matmul_a(0, 1, middle, None)
-            quantise_middle(1)
-            flip_middle(2)
-            load_p(nc.sync, 1)
-            for j in range(KERNEL):
-                for edge in range(2):
-                    place_edge_g(1, edge, j)
-            diff[0] = subtract_p(0)
-            a_bf[1] = matmul_a(1, 1, middle, None)
-            quantise_a(0, 1, a_bf[0])
-            pack_edges(1)
+            load_p(nc.scalar, 1)
+            for edge in range(2):
+                place_edge_g(0, edge, 1)
+            place_row_ends(0, grouped[2], ends)
+            for edge in range(2):
+                place_edge_g(1, edge, 0)
             pack_rows(3)
+            flip_middle(3)
+            quantise_middle(1)
             flip_g(G_UP)
             flip_g(G_DOWN)
-            quantise_middle(2)
-            edge_grouped = flip_u(edge_rows[:])
-            p_grouped[0] = regroup_p(diff[0])
-            quantise_a(1, 1, a_bf[1])
-            a_bf[2] = matmul_a(2, 1, middle, None)
+            a_bf[1] = matmul_a(1, 1, middle, None)
+            edges = quantise_u(ends, "edges")
+            pack_rows(4)
+            quantise_a(0, 1, a_bf[0])
+            grouped[5] = shift_words(grouped[3])
+            for edge in range(2):
+                place_edge_g(1, edge, 1)
+            place_row_ends(1, grouped[5], ends)
+            for half in range(HALVES):
+                for edge in range(2):
+                    place_edge_g(half, edge, 2)
+            quantise_middle(3)
+            flip_middle(4)
+            a_bf[2] = matmul_a(3, 1, middle, None)
             quantise_g(G_UP)
             quantise_g(G_DOWN)
-            edges = quantise_u(edge_grouped, "edges")
+            diff[0] = subtract_p(0)
+            quantise_a(1, 1, a_bf[1])
+            quantise_middle(4)
+            p_grouped[0] = regroup_p(diff[0])
             diff[1] = subtract_p(1)
-            quantise_a(2, 1, a_bf[2])
+            quantise_a(3, 1, a_bf[2])
             quantise_p(0, p_grouped[0])
 
-            for unit in range(UNITS):
-                ahead = unit + KERNEL
-                if ahead < UNITS:
-                    flip_middle(ahead)
-                if unit + 1 < UNITS:
-                    p_grouped[unit + 1] = regroup_p(diff[unit + 1])
+            for step in range(UNITS):
+                unit = ORDER[step]
+                if step + 1 < UNITS:
+                    p_grouped[step + 1] = regroup_p(diff[step + 1])
                 a_bf[0] = matmul_a(unit, 0, middle, edges)
-                if ahead < UNITS:
-                    quantise_middle(ahead)
-                if ahead + 1 < UNITS:
-                    pack_rows(ahead + 1)
-                if unit + 2 < UNITS:
-                    diff[unit + 2] = subtract_p(unit + 2)
+                if step + 4 < UNITS:
+                    quantise_middle(ORDER[step + 4])
+                if step + 2 < UNITS:
+                    diff[step + 2] = subtract_p(step + 2)
                 quantise_a(unit, 0, a_bf[0])
-                if unit + 1 < UNITS:
-                    quantise_p(unit + 1, p_grouped[unit + 1])
+                if step + 1 < UNITS:
+                    quantise_p(step + 1, p_grouped[step + 1])
                 a_bf[2] = matmul_a(unit, 2, middle, edges)
                 quantise_a(unit, 2, a_bf[2])
-                if ahead < UNITS:
+                if step + 3 < UNITS:
+                    ahead = ORDER[step + 3]
                     a_bf[1] = matmul_a(ahead, 1, middle, None)
                     quantise_a(ahead, 1, a_bf[1])
-                if unit > 1:
-                    second_matmul(unit - 2)
+                if step > 1:
+                    second_matmul(step - 2)
             second_matmul(UNITS - 2)
             second_matmul(UNITS - 1)
 

@@ -56,8 +56,9 @@ def tile_convexrelucnn_t_kernel(tc, x, G, v, w, out):
         g_rows = keep.tile([P, M_TILES, 2, G_ROWS * RUN], BF16)
         g_grouped = keep.tile([P, 3, GM * 4], BF16, align_bytes=64)
         g_mx = keep.tile([P, 3, G_WORDS], U32, align_bytes=64)
-        edge_codes = keep.tile([P, HALVES, 2, KERNEL, GM], U32, align_bytes=64)
-        edge_scales = keep.tile([P, HALVES, KERNEL, GM], U8, align_bytes=64)
+        edge_mx = keep.tile([P, 2, KERNEL, G_WORDS], U32, align_bytes=64)
+        edges_second = keep.tile([P, COLS], U32, align_bytes=64)
+        edges_second_scales = keep.tile([P, COLS], U8, align_bytes=64)
         v_sb = keep.tile([P, M_TILES, K, O], BF16)
         w_sb = keep.tile([P, M_TILES, K, O], BF16)
         p_codes = keep.tile([P, M_TILES, KERNEL, KERNEL, O], U32, align_bytes=64)
@@ -124,17 +125,31 @@ def tile_convexrelucnn_t_kernel(tc, x, G, v, w, out):
                 in_=g_grouped[:, form, :],
             )
 
-        def place_edge_g(half, edge, j):
-            slot, row = edge_slot(half, edge, j), (HO - 1) * edge
-            to_scale, from_scale = 32 * (slot // 4) + slot % 4, 32 * (row // 4) + row % 4
-            nc.sync.dma_start(
-                out=edge_codes[8 * slot : 8 * slot + 8, half, edge, j, :].bitcast(I32),
-                in_=g_mx[8 * row : 8 * row + 8, G_PLAIN, :GM].bitcast(I32),
-            )
-            nc.sync.dma_start(
-                out=edge_scales[to_scale : to_scale + 1, half, j, :].bitcast(I32),
-                in_=g_mx[from_scale : from_scale + 1, G_PLAIN, GM:].bitcast(I32),
-            )
+        def place_edge_g(edge, j):
+            form = edge_mx[:, edge, j, :].bitcast(I32)
+            plain = g_mx[:, G_PLAIN, :].bitcast(I32)
+            slot = SLOT_WORDS * edge_slot(0, edge, j)
+            if edge == 0:
+                nc.sync.dma_start(out=form[slot : slot + 8, :], in_=plain[0:8, :])
+            else:
+                nc.sync.dma_start(out=form[slot : slot + 8, :GM], in_=plain[P - 8 : P, :GM])
+                scale = 32 * j + HALVES * edge
+                nc.sync.dma_start(out=form[scale : scale + 1, GM:], in_=plain[99:100, GM:])
+
+        def move_edges(edges):
+            codes, scales = edges
+            for low, high in ((0, 64), (64, 96)):
+                nc.sync.dma_start(
+                    out=edges_second[low:high, :].bitcast(I32),
+                    in_=codes[low + SLOT_WORDS : high + SLOT_WORDS, :].bitcast(I32),
+                )
+            for edge in range(2):
+                low = HALVES * edge
+                nc.sync.dma_start(
+                    out=edges_second_scales[low:P:32, :].bitcast(I32),
+                    in_=scales[low + 1 : P : 32, :].bitcast(I32),
+                )
+            return edges_second, edges_second_scales
 
         def row_runs(tiles, j, image_rows):
             return (
@@ -240,9 +255,8 @@ def tile_convexrelucnn_t_kernel(tc, x, G, v, w, out):
 
         def edge_pass(bank, unit, edge, mt, u_mx):
             half, j = divmod(unit, KERNEL)
-            first_pass(
-                bank, edge_codes[:, half, edge, j, :], edge_scales[:, half, j, :], mt, u_mx, False, True
-            )
+            form = edge_mx[:, edge, j, :]
+            first_pass(bank, form[:, :GM], form[:, GM:].bitcast(U8), mt, u_mx[half], False, True)
 
         def matmul_a(unit, i, middle, edges):
             a_bf = work.tile([P, M_TILES, COLS], BF16, name="a_bf", bufs=4, align_bytes=64)
@@ -341,11 +355,10 @@ def tile_convexrelucnn_t_kernel(tc, x, G, v, w, out):
             make_identity(nc, ident[:])
             nc.vector.memset(g_rows[:, :, :, :RUN].bitcast(U32), 0)
             nc.vector.memset(g_rows[:, :, :, (HO + 1) * RUN :].bitcast(U32), 0)
-            nc.vector.memset(edge_scales[:].rearrange("p h j m -> p (h j m)").bitcast(U32), 0)
-            nc.vector.memset(edge_codes[:, 0].rearrange("p e j m -> p (e j m)"), 0)
-            for edge in range(2):
-                for j in range(KERNEL):
-                    nc.gpsimd.memset(edge_codes[:, 1, edge, j, :], 0)
+            nc.vector.memset(g_mx[:, G_PLAIN, GM:], 0)
+            nc.vector.memset(edge_mx[:].rearrange("p e j f -> p (e j f)"), 0)
+            nc.gpsimd.memset(edges_second[96:, :], 0)
+            nc.gpsimd.memset(edges_second_scales[:].bitcast(U32), 0)
 
             grouped, middle, diff, p_grouped = {}, {}, {}, {}
 
@@ -367,17 +380,15 @@ def tile_convexrelucnn_t_kernel(tc, x, G, v, w, out):
             ends = flip_u(edge_rows[:])
             quantise_middle(0)
             quantise_g(G_PLAIN)
-            for edge in range(2):
-                place_edge_g(0, edge, 0)
+            for j in range(KERNEL):
+                place_edge_g(0, j)
+            place_edge_g(1, 0)
             grouped[2] = shift_words(grouped[0])
+            place_edge_g(1, 1)
+            place_row_ends(0, grouped[2], ends)
+            load_p(nc.sync, 1)
             a_bf = {}
             a_bf[0] = matmul_a(0, 1, middle, None)
-            load_p(nc.scalar, 1)
-            for edge in range(2):
-                place_edge_g(0, edge, 1)
-            place_row_ends(0, grouped[2], ends)
-            for edge in range(2):
-                place_edge_g(1, edge, 0)
             pack_rows(3)
             flip_middle(3)
             quantise_middle(1)
@@ -387,22 +398,19 @@ def tile_convexrelucnn_t_kernel(tc, x, G, v, w, out):
             edges = quantise_u(ends, "edges")
             pack_rows(4)
             quantise_a(0, 1, a_bf[0])
+            edges = (edges, move_edges(edges))
             grouped[5] = shift_words(grouped[3])
-            for edge in range(2):
-                place_edge_g(1, edge, 1)
             place_row_ends(1, grouped[5], ends)
-            for half in range(HALVES):
-                for edge in range(2):
-                    place_edge_g(half, edge, 2)
+            place_edge_g(1, 2)
+            diff[0] = subtract_p(0)
             quantise_middle(3)
             flip_middle(4)
             a_bf[2] = matmul_a(3, 1, middle, None)
             quantise_g(G_UP)
             quantise_g(G_DOWN)
-            diff[0] = subtract_p(0)
             quantise_a(1, 1, a_bf[1])
-            quantise_middle(4)
             p_grouped[0] = regroup_p(diff[0])
+            quantise_middle(4)
             diff[1] = subtract_p(1)
             quantise_a(3, 1, a_bf[2])
             quantise_p(0, p_grouped[0])
@@ -412,13 +420,13 @@ def tile_convexrelucnn_t_kernel(tc, x, G, v, w, out):
                 if step + 1 < UNITS:
                     p_grouped[step + 1] = regroup_p(diff[step + 1])
                 a_bf[0] = matmul_a(unit, 0, middle, edges)
-                if step + 4 < UNITS:
-                    quantise_middle(ORDER[step + 4])
                 if step + 2 < UNITS:
                     diff[step + 2] = subtract_p(step + 2)
                 quantise_a(unit, 0, a_bf[0])
                 if step + 1 < UNITS:
                     quantise_p(step + 1, p_grouped[step + 1])
+                if step + 4 < UNITS:
+                    quantise_middle(ORDER[step + 4])
                 a_bf[2] = matmul_a(unit, 2, middle, edges)
                 quantise_a(unit, 2, a_bf[2])
                 if step + 3 < UNITS:

@@ -351,7 +351,6 @@ def tile_convexrelucnn_t_kernel(tc, x, G, v, w, out):
             load_x(2, 2)
             nc.sync.dma_start(out=g_sb[:], in_=G.rearrange("(t p) n -> p t n", p=P))
             load_x(ROW_TILES, ROW_TILES)
-            load_p(nc.sync, 0)
             make_identity(nc, ident[:])
             nc.vector.memset(g_rows[:, :, :, :RUN].bitcast(U32), 0)
             nc.vector.memset(g_rows[:, :, :, (HO + 1) * RUN :].bitcast(U32), 0)
@@ -359,6 +358,8 @@ def tile_convexrelucnn_t_kernel(tc, x, G, v, w, out):
             nc.vector.memset(edge_mx[:].rearrange("p e j f -> p (e j f)"), 0)
             nc.gpsimd.memset(edges_second[96:, :], 0)
             nc.gpsimd.memset(edges_second_scales[:].bitcast(U32), 0)
+            for mt in range(M_TILES):
+                load_p(nc.gpsimd, mt)
 
             grouped, middle, diff, p_grouped = {}, {}, {}, {}
 
@@ -370,6 +371,7 @@ def tile_convexrelucnn_t_kernel(tc, x, G, v, w, out):
 
             pack_rows(0, parts=2)
             flip_middle(0)
+            grouped[2] = shift_words(grouped[0])
             pack_g()
             flip_g(G_PLAIN)
             pack_rows(1)
@@ -380,13 +382,10 @@ def tile_convexrelucnn_t_kernel(tc, x, G, v, w, out):
             ends = flip_u(edge_rows[:])
             quantise_middle(0)
             quantise_g(G_PLAIN)
-            for j in range(KERNEL):
-                place_edge_g(0, j)
-            place_edge_g(1, 0)
-            grouped[2] = shift_words(grouped[0])
-            place_edge_g(1, 1)
+            for j in range(2):
+                for edge in range(2):
+                    place_edge_g(edge, j)
             place_row_ends(0, grouped[2], ends)
-            load_p(nc.sync, 1)
             a_bf = {}
             a_bf[0] = matmul_a(0, 1, middle, None)
             pack_rows(3)
@@ -398,10 +397,11 @@ def tile_convexrelucnn_t_kernel(tc, x, G, v, w, out):
             edges = quantise_u(ends, "edges")
             pack_rows(4)
             quantise_a(0, 1, a_bf[0])
-            edges = (edges, move_edges(edges))
             grouped[5] = shift_words(grouped[3])
+            edges = (edges, move_edges(edges))
             place_row_ends(1, grouped[5], ends)
-            place_edge_g(1, 2)
+            for edge in range(2):
+                place_edge_g(edge, 2)
             diff[0] = subtract_p(0)
             quantise_middle(3)
             flip_middle(4)

@@ -13,6 +13,8 @@ FP8X4 = mybir.dt.float8_e4m3fn_x4
 P = 128
 B, C, H, W = 256, 4, 18, 34
 KERNEL = 3
+WINDOWS = KERNEL * KERNEL
+PAIRS = 9
 HO, WO = H - KERNEL + 1, W - KERNEL + 1
 L = HO * WO
 M, O = 256, 128
@@ -27,6 +29,7 @@ X_PITCH = 624
 UNITS = HALVES * KERNEL
 BANK = 512
 
+RUN_O = 8
 SLOTS = 16
 RUN = WO // 2
 SLOT_WORDS = RUN // 2
@@ -61,8 +64,8 @@ def tile_convexrelucnn_t_kernel(tc, x, G, v, w, out):
         edges_second_scales = keep.tile([P, COLS], U8, align_bytes=64)
         v_sb = keep.tile([P, M_TILES, K, O], BF16)
         w_sb = keep.tile([P, M_TILES, K, O], BF16)
-        p_codes = keep.tile([P, M_TILES, KERNEL, KERNEL, O], U32, align_bytes=64)
-        p_scales = keep.tile([P, M_TILES, KERNEL, KERNEL, O], U8, align_bytes=64)
+        p_codes = keep.tile([P, M_TILES, WINDOWS, O], U32, align_bytes=64)
+        p_scales = keep.tile([P, M_TILES, WINDOWS, O], U8, align_bytes=64)
         a_codes = keep.tile([P, UNITS, KERNEL, M_TILES * P], U32, align_bytes=64)
         a_scales = keep.tile([P, UNITS, KERNEL, M_TILES * P], U8, align_bytes=64)
         ident = keep.tile([P, P], F32)
@@ -158,10 +161,10 @@ def tile_convexrelucnn_t_kernel(tc, x, G, v, w, out):
                 .rearrange("p t h (u e) -> p u t h e", u=2)
             )
 
-        def pack_rows(unit, parts=1):
+        def pack_rows(unit, counts=(ROW_TILES,)):
             half, j = divmod(unit, KERNEL)
-            count = ROW_TILES // parts
-            for first in range(0, ROW_TILES, count):
+            for part, count in enumerate(counts):
+                first = sum(counts[:part])
                 tiles = slice(half * ROW_TILES + first, half * ROW_TILES + first + count)
                 nc.vector.tensor_copy(
                     out=rows[:, unit, :, first : first + count].rearrange(
@@ -270,10 +273,7 @@ def tile_convexrelucnn_t_kernel(tc, x, G, v, w, out):
                 else:
                     middle_pass(bank, G_DOWN, mt, middle[unit], False)
                     edge_pass(bank, unit, 1, mt, edges)
-                if False:
-                    nc.vector.tensor_copy(out=a_bf[:, mt, :], in_=bank[:])
-                else:
-                    nc.scalar.copy(out=a_bf[:, mt, :], in_=bank[:])
+                nc.scalar.copy(out=a_bf[:, mt, :], in_=bank[:])
             return a_bf
 
         def quantise_a(unit, i, a_bf):
@@ -283,38 +283,43 @@ def tile_convexrelucnn_t_kernel(tc, x, G, v, w, out):
                 in_=a_bf[:].rearrange("p t c -> p (t c)"),
             )
 
-        def rows_of_j(sbuf, mt, j):
-            return sbuf[:, mt].rearrange("p (c i r) o -> p c i r o", c=C, i=KERNEL)[
-                :, :, :, j, :
-            ]
+        def subtract_p(pair):
+            p_grouped = work.tile([P, 2, O, C], BF16, name="p_grouped", bufs=4, align_bytes=64)
+            place = 0
+            while place < 2:
+                mt, first = divmod(2 * pair + place, WINDOWS)
+                count = min(2 - place, WINDOWS - first)
 
-        def subtract_p(unit):
-            mt, j = divmod(unit, KERNEL)
-            diff = work.tile([P, C, KERNEL, O], BF16, name="diff")
-            nc.vector.tensor_tensor(
-                out=diff[:],
-                in0=rows_of_j(v_sb, mt, j),
-                in1=rows_of_j(w_sb, mt, j),
-                op=mybir.AluOpType.subtract,
-            )
-            return diff
+                def runs(sbuf):
+                    return (
+                        sbuf[:, mt]
+                        .rearrange("p (c k) o -> p c (k o)", c=C)[
+                            :, :, first * O : (first + count) * O
+                        ]
+                        .rearrange("p c (q r) -> p q c r", r=RUN_O)
+                    )
 
-        def regroup_p(diff):
-            p_grouped = work.tile([P, KERNEL, O, C], BF16, name="p_grouped", align_bytes=64)
-            nc.vector.tensor_copy(
-                out=p_grouped[:].rearrange("p i (q r) c -> p i q c r", r=4),
-                in_=diff[:].rearrange("p c i (q r) -> p i q c r", r=4),
-            )
+                nc.vector.tensor_tensor(
+                    out=p_grouped[:, place : place + count]
+                    .rearrange("p k o c -> p (k o) c")
+                    .rearrange("p (q r) c -> p q c r", r=RUN_O),
+                    in0=runs(v_sb),
+                    in1=runs(w_sb),
+                    op=mybir.AluOpType.subtract,
+                )
+                place += count
             return p_grouped
 
-        def quantise_p(unit, p_grouped):
-            mt, j = divmod(unit, KERNEL)
-            for i in (slice(0, 2), slice(2, 3)):
-                nc.vector.quantize_mx(
-                    out=p_codes[:, mt, j, i, :].rearrange("p i o -> p (i o)").bitcast(FP8X4),
-                    scales=p_scales[:, mt, j, i, :].rearrange("p i o -> p (i o)"),
-                    in_=p_grouped[:, i].rearrange("p i o c -> p (i o c)"),
-                )
+        def quantise_p(pair, p_grouped):
+            cols = slice(2 * pair * O, (2 * pair + 2) * O)
+            nc.vector.quantize_mx(
+                out=p_codes[:].rearrange("p t k o -> p (t k o)")[:, cols].bitcast(FP8X4),
+                scales=p_scales[:].rearrange("p t k o -> p (t k o)")[:, cols],
+                in_=p_grouped[:].rearrange("p k o c -> p (k o c)"),
+            )
+
+        def pair_step(pair):
+            return 2 * pair // 3 - 1
 
         def second_pass(half, j, i, mt, start, stop):
             m_cols = slice(mt * P, (mt + 1) * P)
@@ -322,8 +327,8 @@ def tile_convexrelucnn_t_kernel(tc, x, G, v, w, out):
                 out=acc[half][:],
                 lhsT=a_codes[:, half * KERNEL + j, i, m_cols].bitcast(FP8X4),
                 lhsT_scale=a_scales[:, half * KERNEL + j, i, m_cols],
-                rhs=p_codes[:, mt, j, i, :].bitcast(FP8X4),
-                rhs_scale=p_scales[:, mt, j, i, :],
+                rhs=p_codes[:, mt, i * KERNEL + j, :].bitcast(FP8X4),
+                rhs_scale=p_scales[:, mt, i * KERNEL + j, :],
                 start=start,
                 stop=stop,
             )
@@ -331,11 +336,12 @@ def tile_convexrelucnn_t_kernel(tc, x, G, v, w, out):
         passes_done = [0, 0]
 
         def second_matmul(step):
-            for half in range(HALVES):
-                for mt in range(M_TILES):
-                    for j in range(KERNEL):
-                        if max(ORDER.index(half * KERNEL + j), mt * KERNEL + j) == step:
-                            for i in range(KERNEL):
+            for i in (1, 0, 2):
+                for half in range(HALVES):
+                    for mt in range(M_TILES):
+                        for j in range(KERNEL):
+                            pair = (mt * WINDOWS + i * KERNEL + j) // 2
+                            if max(ORDER.index(half * KERNEL + j), pair_step(pair)) == step:
                                 passes_done[half] += 1
                                 second_pass(
                                     half,
@@ -343,14 +349,17 @@ def tile_convexrelucnn_t_kernel(tc, x, G, v, w, out):
                                     i,
                                     mt,
                                     passes_done[half] == 1,
-                                    passes_done[half] == M_TILES * KERNEL * KERNEL,
+                                    passes_done[half] == M_TILES * WINDOWS,
                                 )
 
         with tc.manual_schedule():
-            load_x(0, 2)
+            load_x(0, 1)
+            load_x(1, 1)
             load_x(2, 2)
             nc.sync.dma_start(out=g_sb[:], in_=G.rearrange("(t p) n -> p t n", p=P))
             load_x(ROW_TILES, ROW_TILES)
+            for mt in range(M_TILES):
+                load_p(nc.scalar, mt)
             make_identity(nc, ident[:])
             nc.vector.memset(g_rows[:, :, :, :RUN].bitcast(U32), 0)
             nc.vector.memset(g_rows[:, :, :, (HO + 1) * RUN :].bitcast(U32), 0)
@@ -358,10 +367,8 @@ def tile_convexrelucnn_t_kernel(tc, x, G, v, w, out):
             nc.vector.memset(edge_mx[:].rearrange("p e j f -> p (e j f)"), 0)
             nc.gpsimd.memset(edges_second[96:, :], 0)
             nc.gpsimd.memset(edges_second_scales[:].bitcast(U32), 0)
-            for mt in range(M_TILES):
-                load_p(nc.gpsimd, mt)
 
-            grouped, middle, diff, p_grouped = {}, {}, {}, {}
+            grouped, middle, p_grouped = {}, {}, {}
 
             def flip_middle(unit):
                 grouped[unit] = flip_u(rows[:, unit])
@@ -369,7 +376,7 @@ def tile_convexrelucnn_t_kernel(tc, x, G, v, w, out):
             def quantise_middle(unit):
                 middle[unit] = quantise_u(grouped[unit], "middle")
 
-            pack_rows(0, parts=2)
+            pack_rows(0, counts=(1, 1, 2))
             flip_middle(0)
             grouped[2] = shift_words(grouped[0])
             pack_g()
@@ -382,9 +389,9 @@ def tile_convexrelucnn_t_kernel(tc, x, G, v, w, out):
             ends = flip_u(edge_rows[:])
             quantise_middle(0)
             quantise_g(G_PLAIN)
-            for j in range(2):
-                for edge in range(2):
-                    place_edge_g(edge, j)
+            place_edge_g(0, 0)
+            place_edge_g(1, 0)
+            place_edge_g(0, 1)
             place_row_ends(0, grouped[2], ends)
             a_bf = {}
             a_bf[0] = matmul_a(0, 1, middle, None)
@@ -398,44 +405,48 @@ def tile_convexrelucnn_t_kernel(tc, x, G, v, w, out):
             pack_rows(4)
             quantise_a(0, 1, a_bf[0])
             grouped[5] = shift_words(grouped[3])
+            place_edge_g(1, 1)
             edges = (edges, move_edges(edges))
             place_row_ends(1, grouped[5], ends)
-            for edge in range(2):
-                place_edge_g(edge, 2)
-            diff[0] = subtract_p(0)
+            place_edge_g(0, 2)
+            place_edge_g(1, 2)
+            p_grouped[0] = subtract_p(0)
             quantise_middle(3)
             flip_middle(4)
             a_bf[2] = matmul_a(3, 1, middle, None)
             quantise_g(G_UP)
             quantise_g(G_DOWN)
             quantise_a(1, 1, a_bf[1])
-            p_grouped[0] = regroup_p(diff[0])
-            quantise_middle(4)
-            diff[1] = subtract_p(1)
-            quantise_a(3, 1, a_bf[2])
             quantise_p(0, p_grouped[0])
+            quantise_middle(4)
+            p_grouped[1] = subtract_p(1)
+            quantise_a(3, 1, a_bf[2])
+            quantise_p(1, p_grouped[1])
 
             for step in range(UNITS):
                 unit = ORDER[step]
-                if step + 1 < UNITS:
-                    p_grouped[step + 1] = regroup_p(diff[step + 1])
+                pairs = [pair for pair in range(PAIRS) if pair_step(pair) == step]
+                for pair in pairs[:1]:
+                    p_grouped[pair] = subtract_p(pair)
                 a_bf[0] = matmul_a(unit, 0, middle, edges)
-                if step + 2 < UNITS:
-                    diff[step + 2] = subtract_p(step + 2)
-                quantise_a(unit, 0, a_bf[0])
-                if step + 1 < UNITS:
-                    quantise_p(step + 1, p_grouped[step + 1])
                 if step + 4 < UNITS:
                     quantise_middle(ORDER[step + 4])
+                for pair in pairs[1:]:
+                    p_grouped[pair] = subtract_p(pair)
+                quantise_a(unit, 0, a_bf[0])
+                for pair in pairs:
+                    quantise_p(pair, p_grouped[pair])
                 a_bf[2] = matmul_a(unit, 2, middle, edges)
+                if step == UNITS - 1:
+                    second_matmul(step - 2)
+                    second_matmul(step - 1)
                 quantise_a(unit, 2, a_bf[2])
                 if step + 3 < UNITS:
                     ahead = ORDER[step + 3]
                     a_bf[1] = matmul_a(ahead, 1, middle, None)
                     quantise_a(ahead, 1, a_bf[1])
-                if step > 1:
+                if 1 < step < UNITS - 1:
                     second_matmul(step - 2)
-            second_matmul(UNITS - 2)
             second_matmul(UNITS - 1)
 
             result0 = work.tile([P, O], F32, name="result0")

@@ -217,10 +217,10 @@ def tile_convexrelucnn_t_kernel(tc, x, G, v, w, out):
 
         def shift_words(source):
             shifted = new_grouped()
-            for low, high in ((0, P // 2), (P // 2, P - 1)):
+            for first, step in ((0, 4), (1, 4), (2, 4), (3, SLOT_WORDS)):
                 nc.sync.dma_start(
-                    out=shifted[low:high, :].bitcast(I32),
-                    in_=source[low + 1 : high + 1, :].bitcast(I32),
+                    out=shifted[first::step, :].bitcast(I32),
+                    in_=source[first + 1 :: step, :].bitcast(I32),
                 )
             return shifted
 
@@ -358,8 +358,7 @@ def tile_convexrelucnn_t_kernel(tc, x, G, v, w, out):
             load_x(2, 2)
             nc.sync.dma_start(out=g_sb[:], in_=G.rearrange("(t p) n -> p t n", p=P))
             load_x(ROW_TILES, ROW_TILES)
-            for mt in range(M_TILES):
-                load_p(nc.scalar, mt)
+            load_p(nc.sync, 0)
             make_identity(nc, ident[:])
             nc.vector.memset(g_rows[:, :, :, :RUN].bitcast(U32), 0)
             nc.vector.memset(g_rows[:, :, :, (HO + 1) * RUN :].bitcast(U32), 0)
@@ -391,8 +390,9 @@ def tile_convexrelucnn_t_kernel(tc, x, G, v, w, out):
             quantise_g(G_PLAIN)
             place_edge_g(0, 0)
             place_edge_g(1, 0)
-            place_edge_g(0, 1)
             place_row_ends(0, grouped[2], ends)
+            place_edge_g(0, 1)
+            place_edge_g(1, 1)
             a_bf = {}
             a_bf[0] = matmul_a(0, 1, middle, None)
             pack_rows(3)
@@ -405,15 +405,15 @@ def tile_convexrelucnn_t_kernel(tc, x, G, v, w, out):
             pack_rows(4)
             quantise_a(0, 1, a_bf[0])
             grouped[5] = shift_words(grouped[3])
-            place_edge_g(1, 1)
-            edges = (edges, move_edges(edges))
             place_row_ends(1, grouped[5], ends)
+            edges = (edges, move_edges(edges))
             place_edge_g(0, 2)
             place_edge_g(1, 2)
             p_grouped[0] = subtract_p(0)
             quantise_middle(3)
             flip_middle(4)
             a_bf[2] = matmul_a(3, 1, middle, None)
+            load_p(nc.scalar, 1)
             quantise_g(G_UP)
             quantise_g(G_DOWN)
             quantise_a(1, 1, a_bf[1])

@@ -69,7 +69,9 @@ def tile_convexrelucnn_t_kernel(tc, x, G, v, w, out):
         a_codes = keep.tile([P, UNITS, KERNEL, M_TILES * P], U32, align_bytes=64)
         a_scales = keep.tile([P, UNITS, KERNEL, M_TILES * P], U8, align_bytes=64)
         ident = keep.tile([P, P], F32)
-        acc = [sums.tile([P, O], F32, name="acc%d" % half) for half in range(HALVES)]
+        idle_rows = keep.tile([P, BANK], BF16)
+        acc_banks = [sums.tile([P, BANK], F32, name="acc%d" % half) for half in range(HALVES)]
+        acc = [bank[:, :O] for bank in acc_banks]
 
         x_rows = x.rearrange("b c h w -> (b c) (h w)").rearrange(
             "(t p) f -> p t f", p=P
@@ -83,6 +85,16 @@ def tile_convexrelucnn_t_kernel(tc, x, G, v, w, out):
         def load_p(queue, mt):
             queue.dma_start(out=v_sb[:, mt], in_=v[mt * P : (mt + 1) * P])
             queue.dma_start(out=w_sb[:, mt], in_=w[mt * P : (mt + 1) * P])
+
+        def keep_warm(count):
+            for repeat in range(count):
+                nc.tensor.matmul(
+                    out=acc_banks[1][:],
+                    lhsT=idle_rows[:, :P],
+                    rhs=idle_rows[:],
+                    start=True,
+                    stop=True,
+                )
 
         def flip_words(words):
             bank = banks.tile([P, BANK], F32, name="bank")
@@ -319,12 +331,12 @@ def tile_convexrelucnn_t_kernel(tc, x, G, v, w, out):
             )
 
         def pair_step(pair):
-            return 2 * pair // 3 - 1
+            return 2 * pair // 3 - 1 + (pair == 4)
 
         def second_pass(half, j, i, mt, start, stop):
             m_cols = slice(mt * P, (mt + 1) * P)
             nc.tensor.matmul_mx(
-                out=acc[half][:],
+                out=acc[half],
                 lhsT=a_codes[:, half * KERNEL + j, i, m_cols].bitcast(FP8X4),
                 lhsT_scale=a_scales[:, half * KERNEL + j, i, m_cols],
                 rhs=p_codes[:, mt, i * KERNEL + j, :].bitcast(FP8X4),
@@ -355,11 +367,14 @@ def tile_convexrelucnn_t_kernel(tc, x, G, v, w, out):
         with tc.manual_schedule():
             load_x(0, 1)
             load_x(1, 1)
-            load_x(2, 2)
+            load_x(2, 1)
+            load_x(3, 1)
             nc.sync.dma_start(out=g_sb[:], in_=G.rearrange("(t p) n -> p t n", p=P))
             load_x(ROW_TILES, ROW_TILES)
             load_p(nc.sync, 0)
+            nc.vector.memset(idle_rows[:].bitcast(U32), 0)
             make_identity(nc, ident[:])
+            keep_warm(6)
             nc.vector.memset(g_rows[:, :, :, :RUN].bitcast(U32), 0)
             nc.vector.memset(g_rows[:, :, :, (HO + 1) * RUN :].bitcast(U32), 0)
             nc.vector.memset(g_mx[:, G_PLAIN, GM:], 0)
@@ -375,9 +390,10 @@ def tile_convexrelucnn_t_kernel(tc, x, G, v, w, out):
             def quantise_middle(unit):
                 middle[unit] = quantise_u(grouped[unit], "middle")
 
-            pack_rows(0, counts=(1, 1, 2))
+            pack_rows(0, counts=(1, 1, 1, 1))
             flip_middle(0)
             grouped[2] = shift_words(grouped[0])
+            keep_warm(2)
             pack_g()
             flip_g(G_PLAIN)
             pack_rows(1)
@@ -404,16 +420,17 @@ def tile_convexrelucnn_t_kernel(tc, x, G, v, w, out):
             edges = quantise_u(ends, "edges")
             pack_rows(4)
             quantise_a(0, 1, a_bf[0])
+            nc.sync.dma_start(out=v_sb[:, 1], in_=v[P:])
             grouped[5] = shift_words(grouped[3])
             place_row_ends(1, grouped[5], ends)
             edges = (edges, move_edges(edges))
+            nc.sync.dma_start(out=w_sb[:, 1], in_=w[P:])
             place_edge_g(0, 2)
             place_edge_g(1, 2)
             p_grouped[0] = subtract_p(0)
             quantise_middle(3)
             flip_middle(4)
             a_bf[2] = matmul_a(3, 1, middle, None)
-            load_p(nc.scalar, 1)
             quantise_g(G_UP)
             quantise_g(G_DOWN)
             quantise_a(1, 1, a_bf[1])
@@ -451,7 +468,7 @@ def tile_convexrelucnn_t_kernel(tc, x, G, v, w, out):
 
             result0 = work.tile([P, O], F32, name="result0")
             result1 = work.tile([P, O], F32, name="result1")
-            nc.scalar.copy(out=result0[:], in_=acc[0][:])
-            nc.vector.tensor_copy(out=result1[:], in_=acc[1][:])
+            nc.scalar.copy(out=result0[:], in_=acc[0])
+            nc.vector.tensor_copy(out=result1[:], in_=acc[1])
             nc.sync.dma_start(out=out[:P, :], in_=result0[:])
             nc.scalar.dma_start(out=out[P:, :], in_=result1[:])

from contextlib import ExitStack

import concourse.mybir as mybir
from concourse.masks import make_identity

BF16 = mybir.dt.bfloat16
F32 = mybir.dt.float32
I32 = mybir.dt.int32
U32 = mybir.dt.uint32
U8 = mybir.dt.uint8
FP8X4 = mybir.dt.float8_e4m3fn_x4

P = 128
B, C, H, W = 256, 4, 18, 34
KERNEL = 3
WINDOWS = KERNEL * KERNEL
PAIRS = 9
HO, WO = H - KERNEL + 1, W - KERNEL + 1
L = HO * WO
M, O = 256, 128
K = C * KERNEL * KERNEL
FLOPS = 2 * B * K * L * M + 2 * B * K * M * O

HALVES = 2
ROW_TILES = 4
COLS = ROW_TILES * P
M_TILES = M // P
X_PITCH = 624
UNITS = HALVES * KERNEL
BANK = 512

RUN_O = 8
SLOTS = 16
RUN = WO // 2
SLOT_WORDS = RUN // 2
G_ROWS = HO + 2
KERNEL_SLOTS = 2 * HALVES
GM = M_TILES * P
G_WORDS = GM + GM // 4

ORDER = (0, 1, 3, 4, 2, 5)

G_DOWN, G_PLAIN, G_UP = 0, 1, 2


def tile_convexrelucnn_t_kernel(tc, x, G, v, w, out):
    nc = tc.nc

    with ExitStack() as pools:
        keep = pools.enter_context(tc.tile_pool(name="keep", bufs=1))
        work = pools.enter_context(tc.tile_pool(name="work", bufs=2))
        banks = pools.enter_context(tc.psum_pool(name="banks", bufs=6))
        sums = pools.enter_context(tc.psum_pool(name="sums", bufs=1))

        x_sb = keep.tile([P, HALVES * ROW_TILES, X_PITCH], BF16)
        rows = keep.tile([P, UNITS, 2, ROW_TILES, SLOTS * RUN], BF16)
        edge_rows = keep.tile([P, 2, ROW_TILES, SLOTS * RUN], BF16)
        g_sb = keep.tile([P, M_TILES, L], BF16)
        g_rows = keep.tile([P, M_TILES, 2, G_ROWS * RUN], BF16)
        g_grouped = keep.tile([P, 3, GM * 4], BF16, align_bytes=64)
        g_mx = keep.tile([P, 3, G_WORDS], U32, align_bytes=64)
        edge_mx = keep.tile([P, 2, KERNEL, G_WORDS], U32, align_bytes=64)
        edges_second = keep.tile([P, COLS], U32, align_bytes=64)
        edges_second_scales = keep.tile([P, COLS], U8, align_bytes=64)
        v_sb = keep.tile([P, M_TILES, K, O], BF16)
        w_sb = keep.tile([P, M_TILES, K, O], BF16)
        p_codes = keep.tile([P, M_TILES, WINDOWS, O], U32, align_bytes=64)
        p_scales = keep.tile([P, M_TILES, WINDOWS, O], U8, align_bytes=64)
        a_codes = keep.tile([P, UNITS, KERNEL, M_TILES * P], U32, align_bytes=64)
        a_scales = keep.tile([P, UNITS, KERNEL, M_TILES * P], U8, align_bytes=64)
        ident = keep.tile([P, P], F32)
        idle_rows = keep.tile([P, BANK], BF16)
        acc_banks = [sums.tile([P, BANK], F32, name="acc%d" % half) for half in range(HALVES)]
        acc = [bank[:, :O] for bank in acc_banks]

        x_rows = x.rearrange("b c h w -> (b c) (h w)").rearrange(
            "(t p) f -> p t f", p=P
        )


        def load_x(first, count):
            tiles = slice(first, first + count)
            nc.sync.dma_start(out=x_sb[:, tiles, : H * W], in_=x_rows[:, tiles, :])

        def load_p(queue, mt):
            queue.dma_start(out=v_sb[:, mt], in_=v[mt * P : (mt + 1) * P])
            queue.dma_start(out=w_sb[:, mt], in_=w[mt * P : (mt + 1) * P])

        def keep_warm(count):
            for repeat in range(count):
                nc.tensor.matmul(
                    out=acc_banks[1][:],
                    lhsT=idle_rows[:, :P],
                    rhs=idle_rows[:],
                    start=True,
                    stop=True,
                )

        def flip_words(words):
            bank = banks.tile([P, BANK], F32, name="bank")
            blocks = bank[:].rearrange("p (r u c) -> p r u c", r=2, u=2)
            for r in range(2):
                for u in range(2):
                    nc.tensor.transpose(blocks[:, r, u, :], words(r, u), ident[:])
            return blocks

        def leave_flip_bank(blocks, grouped_words):
            nc.scalar.copy(
                out=grouped_words, in_=blocks.rearrange("p r u c -> p r c u")
            )

        def pack_g():
            nc.vector.tensor_copy(
                out=g_rows[:, :, :, RUN : (HO + 1) * RUN].rearrange(
                    "p t u (h e) -> p t u h e", e=RUN
                ),
                in_=g_sb[:].rearrange("p t (h u e) -> p t u h e", u=2, e=RUN),
            )

        def flip_g(form):
            words = g_rows[:].rearrange("p t u f -> p (t u f)").bitcast(F32).rearrange(
                "p (t u f) -> p t u f", t=M_TILES, u=2
            )
            start = form * SLOT_WORDS
            blocks = flip_words(lambda mt, u: words[:, mt, u, start : start + P])
            leave_flip_bank(
                blocks,
                g_grouped[:, form, :]
                .bitcast(F32)
                .rearrange("p (r c u) -> p r c u", r=2, u=2),
            )

        def edge_slot(half, edge, j):
            return KERNEL_SLOTS * j + HALVES * edge + half

        def quantise_g(form):
            nc.vector.quantize_mx(
                out=g_mx[:, form, :GM].bitcast(FP8X4),
                scales=g_mx[:, form, GM:].bitcast(U8),
                in_=g_grouped[:, form, :],
            )

        def place_edge_g(edge, j):
            form = edge_mx[:, edge, j, :].bitcast(I32)
            plain = g_mx[:, G_PLAIN, :].bitcast(I32)
            slot = SLOT_WORDS * edge_slot(0, edge, j)
            if edge == 0:
                nc.sync.dma_start(out=form[slot : slot + 8, :], in_=plain[0:8, :])
            else:
                nc.sync.dma_start(out=form[slot : slot + 8, :GM], in_=plain[P - 8 : P, :GM])
                scale = 32 * j + HALVES * edge
                nc.sync.dma_start(out=form[scale : scale + 1, GM:], in_=plain[99:100, GM:])

        def move_edges(edges):
            codes, scales = edges
            for low, high in ((0, 64), (64, 96)):
                nc.sync.dma_start(
                    out=edges_second[low:high, :].bitcast(I32),
                    in_=codes[low + SLOT_WORDS : high + SLOT_WORDS, :].bitcast(I32),
                )
            for edge in range(2):
                low = HALVES * edge
                nc.sync.dma_start(
                    out=edges_second_scales[low:P:32, :].bitcast(I32),
                    in_=scales[low + 1 : P : 32, :].bitcast(I32),
                )
            return edges_second, edges_second_scales

        def row_runs(tiles, j, image_rows):
            return (
                x_sb[:, tiles, : H * W]
                .rearrange("p t (h w) -> p t h w", w=W)[:, :, image_rows, j : j + WO]
                .rearrange("p t h (u e) -> p u t h e", u=2)
            )

        def pack_rows(unit, counts=(ROW_TILES,)):
            half, j = divmod(unit, KERNEL)
            for part, count in enumerate(counts):
                first = sum(counts[:part])
                tiles = slice(half * ROW_TILES + first, half * ROW_TILES + first + count)
                nc.vector.tensor_copy(
                    out=rows[:, unit, :, first : first + count].rearrange(
                        "p u t (h e) -> p u t h e", e=RUN
                    ),
                    in_=row_runs(tiles, j, slice(1, HO + 1)),
                )

        def pack_edges(half):
            slots = edge_rows[:].rearrange("p u t (h e) -> p u t h e", e=RUN)
            for j in range(KERNEL):
                first_slot, last_slot = edge_slot(half, 0, j), edge_slot(half, 1, j)
                nc.vector.tensor_copy(
                    out=slots[:, :, :, first_slot : last_slot + 1 : last_slot - first_slot, :],
                    in_=row_runs(
                        slice(half * ROW_TILES, (half + 1) * ROW_TILES), j, slice(0, H, H - 1)
                    ),
                )

        def new_grouped():
            return work.tile([P, COLS * 4], BF16, name="grouped", bufs=7, align_bytes=64)

        def flip_u(packed):
            words = packed.rearrange("p u t f -> p (u t f)").bitcast(F32).rearrange(
                "p (u t f) -> p u t f", u=2, t=ROW_TILES
            )
            grouped = new_grouped()
            grouped_words = grouped[:].bitcast(F32).rearrange(
                "p (t c u) -> p t c u", t=ROW_TILES, u=2
            )
            for pair in range(ROW_TILES // 2):
                blocks = flip_words(lambda r, u: words[:, u, 2 * pair + r, :])
                leave_flip_bank(blocks, grouped_words[:, 2 * pair : 2 * pair + 2, :, :])
            return grouped

        def pack_row_ends(half):
            first = (KERNEL * KERNEL_SLOTS + 2 * half) * SLOT_WORDS
            x_words = x_sb[:, half * ROW_TILES : (half + 1) * ROW_TILES, : H * W].bitcast(F32)
            nc.vector.tensor_copy(
                out=edge_rows[:]
                .rearrange("p u t f -> p (u t f)")
                .bitcast(F32)
                .rearrange("p (u t f) -> p u t f", u=2, t=ROW_TILES)[
                    :, :, :, first : first + HO
                ],
                in_=x_words.rearrange("p t (h w) -> p t h w", w=W // 2)[
                    :, :, 1 : HO + 1, SLOT_WORDS :: SLOT_WORDS
                ].rearrange("p t h u -> p u t h"),
            )

        def shift_words(source):
            shifted = new_grouped()
            for first, step in ((0, 4), (1, 4), (2, 4), (3, SLOT_WORDS)):
                nc.sync.dma_start(
                    out=shifted[first::step, :].bitcast(I32),
                    in_=source[first + 1 :: step, :].bitcast(I32),
                )
            return shifted

        def place_row_ends(half, shifted, ends):
            first = SLOT_WORDS * (KERNEL * KERNEL_SLOTS + 2 * half)
            nc.sync.dma_start(
                out=shifted[SLOT_WORDS - 1 :: SLOT_WORDS, :].bitcast(I32),
                in_=ends[first : first + HO, :].bitcast(I32),
            )

        def quantise_u(grouped, name):
            codes = work.tile([P, COLS], U32, name=name + "_codes", bufs=UNITS, align_bytes=64)
            scales = work.tile([P, COLS], U8, name=name + "_scales", bufs=UNITS, align_bytes=64)
            nc.vector.quantize_mx(
                out=codes[:].bitcast(FP8X4), scales=scales[:], in_=grouped[:]
            )
            return codes, scales

        def first_pass(bank, g_codes, g_scales, mt, u_mx, start, stop):
            codes, scales = u_mx
            m_cols = slice(mt * P, (mt + 1) * P)
            nc.tensor.matmul_mx(
                out=bank[:],
                lhsT=g_codes[:, m_cols].bitcast(FP8X4),
                lhsT_scale=g_scales[:, m_cols],
                rhs=codes[:].bitcast(FP8X4),
                rhs_scale=scales[:],
                start=start,
                stop=stop,
            )

        def middle_pass(bank, form, mt, u_mx, stop):
            g_scales = g_mx[:, form, GM:].bitcast(U8)
            first_pass(bank, g_mx[:, form, :GM], g_scales, mt, u_mx, True, stop)

        def edge_pass(bank, unit, edge, mt, u_mx):
            half, j = divmod(unit, KERNEL)
            form = edge_mx[:, edge, j, :]
            first_pass(bank, form[:, :GM], form[:, GM:].bitcast(U8), mt, u_mx[half], False, True)

        def matmul_a(unit, i, middle, edges):
            a_bf = work.tile([P, M_TILES, COLS], BF16, name="a_bf", bufs=4, align_bytes=64)
            for mt in range(M_TILES):
                bank = banks.tile([P, BANK], F32, name="bank")
                if i == 1:
                    middle_pass(bank, G_PLAIN, mt, middle[unit], True)
                elif i == 0:
                    middle_pass(bank, G_UP, mt, middle[unit], False)
                    edge_pass(bank, unit, 0, mt, edges)
                else:
                    middle_pass(bank, G_DOWN, mt, middle[unit], False)
                    edge_pass(bank, unit, 1, mt, edges)
                nc.scalar.copy(out=a_bf[:, mt, :], in_=bank[:])
            return a_bf

        def quantise_a(unit, i, a_bf):
            nc.vector.quantize_mx(
                out=a_codes[:, unit, i, :].bitcast(FP8X4),
                scales=a_scales[:, unit, i, :],
                in_=a_bf[:].rearrange("p t c -> p (t c)"),
            )

        def subtract_p(pair):
            p_grouped = work.tile([P, 2, O, C], BF16, name="p_grouped", bufs=4, align_bytes=64)
            place = 0
            while place < 2:
                mt, first = divmod(2 * pair + place, WINDOWS)
                count = min(2 - place, WINDOWS - first)

                def runs(sbuf):
                    return (
                        sbuf[:, mt]
                        .rearrange("p (c k) o -> p c (k o)", c=C)[
                            :, :, first * O : (first + count) * O
                        ]
                        .rearrange("p c (q r) -> p q c r", r=RUN_O)
                    )

                nc.vector.tensor_tensor(
                    out=p_grouped[:, place : place + count]
                    .rearrange("p k o c -> p (k o) c")
                    .rearrange("p (q r) c -> p q c r", r=RUN_O),
                    in0=runs(v_sb),
                    in1=runs(w_sb),
                    op=mybir.AluOpType.subtract,
                )
                place += count
            return p_grouped

        def quantise_p(pair, p_grouped):
            cols = slice(2 * pair * O, (2 * pair + 2) * O)
            nc.vector.quantize_mx(
                out=p_codes[:].rearrange("p t k o -> p (t k o)")[:, cols].bitcast(FP8X4),
                scales=p_scales[:].rearrange("p t k o -> p (t k o)")[:, cols],
                in_=p_grouped[:].rearrange("p k o c -> p (k o c)"),
            )

        def pair_step(pair):
            return 2 * pair // 3 - 1 + (pair == 4)

        def second_pass(half, j, i, mt, start, stop):
            m_cols = slice(mt * P, (mt + 1) * P)
            nc.tensor.matmul_mx(
                out=acc[half],
                lhsT=a_codes[:, half * KERNEL + j, i, m_cols].bitcast(FP8X4),
                lhsT_scale=a_scales[:, half * KERNEL + j, i, m_cols],
                rhs=p_codes[:, mt, i * KERNEL + j, :].bitcast(FP8X4),
                rhs_scale=p_scales[:, mt, i * KERNEL + j, :],
                start=start,
                stop=stop,
            )

        passes_done = [0, 0]

        def second_matmul(step):
            for i in (1, 0, 2):
                for half in range(HALVES):
                    for mt in range(M_TILES):
                        for j in range(KERNEL):
                            pair = (mt * WINDOWS + i * KERNEL + j) // 2
                            if max(ORDER.index(half * KERNEL + j), pair_step(pair)) == step:
                                passes_done[half] += 1
                                second_pass(
                                    half,
                                    j,
                                    i,
                                    mt,
                                    passes_done[half] == 1,
                                    passes_done[half] == M_TILES * WINDOWS,
                                )

        with tc.manual_schedule():
            load_x(0, 1)
            load_x(1, 1)
            load_x(2, 1)
            load_x(3, 1)
            nc.sync.dma_start(out=g_sb[:], in_=G.rearrange("(t p) n -> p t n", p=P))
            load_x(ROW_TILES, ROW_TILES)
            load_p(nc.sync, 0)
            nc.vector.memset(idle_rows[:].bitcast(U32), 0)
            make_identity(nc, ident[:])
            keep_warm(6)
            nc.vector.memset(g_rows[:, :, :, :RUN].bitcast(U32), 0)
            nc.vector.memset(g_rows[:, :, :, (HO + 1) * RUN :].bitcast(U32), 0)
            nc.vector.memset(g_mx[:, G_PLAIN, GM:], 0)
            nc.vector.memset(edge_mx[:].rearrange("p e j f -> p (e j f)"), 0)
            nc.gpsimd.memset(edges_second[96:, :], 0)
            nc.gpsimd.memset(edges_second_scales[:].bitcast(U32), 0)

            grouped, middle, p_grouped = {}, {}, {}

            def flip_middle(unit):
                grouped[unit] = flip_u(rows[:, unit])

            def quantise_middle(unit):
                middle[unit] = quantise_u(grouped[unit], "middle")

            pack_rows(0, counts=(1, 1, 1, 1))
            flip_middle(0)
            grouped[2] = shift_words(grouped[0])
            keep_warm(2)
            pack_g()
            flip_g(G_PLAIN)
            pack_rows(1)
            flip_middle(1)
            for half in range(HALVES):
                pack_edges(half)
                pack_row_ends(half)
            ends = flip_u(edge_rows[:])
            quantise_middle(0)
            quantise_g(G_PLAIN)
            place_edge_g(0, 0)
            place_edge_g(1, 0)
            place_row_ends(0, grouped[2], ends)
            place_edge_g(0, 1)
            place_edge_g(1, 1)
            a_bf = {}
            a_bf[0] = matmul_a(0, 1, middle, None)
            pack_rows(3)
            flip_middle(3)
            quantise_middle(1)
            flip_g(G_UP)
            flip_g(G_DOWN)
            a_bf[1] = matmul_a(1, 1, middle, None)
            edges = quantise_u(ends, "edges")
            pack_rows(4)
            quantise_a(0, 1, a_bf[0])
            nc.sync.dma_start(out=v_sb[:, 1], in_=v[P:])
            grouped[5] = shift_words(grouped[3])
            place_row_ends(1, grouped[5], ends)
            edges = (edges, move_edges(edges))
            nc.sync.dma_start(out=w_sb[:, 1], in_=w[P:])
            place_edge_g(0, 2)
            place_edge_g(1, 2)
            p_grouped[0] = subtract_p(0)
            quantise_middle(3)
            flip_middle(4)
            a_bf[2] = matmul_a(3, 1, middle, None)
            quantise_g(G_UP)
            quantise_g(G_DOWN)
            quantise_a(1, 1, a_bf[1])
            quantise_p(0, p_grouped[0])
            quantise_middle(4)
            p_grouped[1] = subtract_p(1)
            quantise_a(3, 1, a_bf[2])
            quantise_p(1, p_grouped[1])

            for step in range(UNITS):
                unit = ORDER[step]
                pairs = [pair for pair in range(PAIRS) if pair_step(pair) == step]
                for pair in pairs[:1]:
                    p_grouped[pair] = subtract_p(pair)
                a_bf[0] = matmul_a(unit, 0, middle, edges)
                if step + 4 < UNITS:
                    quantise_middle(ORDER[step + 4])
                for pair in pairs[1:]:
                    p_grouped[pair] = subtract_p(pair)
                quantise_a(unit, 0, a_bf[0])
                for pair in pairs:
                    quantise_p(pair, p_grouped[pair])
                a_bf[2] = matmul_a(unit, 2, middle, edges)
                if step == UNITS - 1:
                    second_matmul(step - 2)
                    second_matmul(step - 1)
                quantise_a(unit, 2, a_bf[2])
                if step + 3 < UNITS:
                    ahead = ORDER[step + 3]
                    a_bf[1] = matmul_a(ahead, 1, middle, None)
                    quantise_a(ahead, 1, a_bf[1])
                if 1 < step < UNITS - 1:
                    second_matmul(step - 2)
            second_matmul(UNITS - 1)

            result0 = work.tile([P, O], F32, name="result0")
            result1 = work.tile([P, O], F32, name="result1")
            nc.scalar.copy(out=result0[:], in_=acc[0])
            nc.vector.tensor_copy(out=result1[:], in_=acc[1])
            nc.sync.dma_start(out=out[:P, :], in_=result0[:])
            nc.scalar.dma_start(out=out[P:, :], in_=result1[:])
